import numpy as np
import ml_dtypes


def mxq(x, axis, fmt="e4m3"):
    dtype, down = {"e4m3": (ml_dtypes.float8_e4m3fn, 7), "e5m2": (ml_dtypes.float8_e5m2, 14)}[fmt]
    v = np.moveaxis(np.asarray(x, np.float32).astype(ml_dtypes.bfloat16).astype(np.float64), axis, -1)
    blocks = v.reshape(v.shape[:-1] + (-1, 32))
    amax = np.abs(blocks).max(-1, keepdims=True)
    byte = np.maximum(np.where(amax > 0, np.frexp(amax)[1] - 1 + 127, 0) - down, 1)
    scale = np.exp2(byte - 127.0)
    codes = (blocks / scale).astype(np.float32).astype(dtype).astype(np.float64)
    return np.moveaxis((codes * scale).reshape(v.shape), -1, axis)


WIDE = False


def mx_kscale(k):
    if not WIDE:
        return np.ones(k)
    levels = np.array([10, -10, 5, -5, 0])
    if k % 512:
        return np.exp2(np.random.permutation(np.resize(levels, k // 32))).repeat(32)
    a = np.empty((k // 512, 16))
    for p in range(k // 512):
        a[p, :8] = np.random.permutation(np.resize(levels, 8))
        for g in range(8):
            far = levels[np.abs(levels - a[p, g]) >= 10]
            a[p, g + 8] = far[np.random.randint(len(far))]
    return np.exp2(a.ravel()).repeat(32)


BF16 = ml_dtypes.bfloat16


def bf(x):
    return np.asarray(x, np.float32).astype(BF16)


def f64(x):
    return np.asarray(x).astype(np.float64)


E2M1 = np.array([0.0, 0.5, 1.0, 1.5, 2.0, 3.0, 4.0, 6.0, -0.0, -0.5, -1.0, -1.5, -2.0, -3.0, -4.0, -6.0])


def pack_weight(w, fmt):
    k, n = w.shape
    w = f64(bf(w)).reshape(k // 32, 32, n)
    amax = np.abs(w).max(1)
    if fmt == "e4m3":
        byte = np.frexp(amax)[1] - 1 + 127 - 7
    else:
        mant, ex = np.frexp(amax / 6.0)
        byte = np.where(mant > 0.5, ex, ex - 1) + 127
    byte = np.clip(np.where(amax > 0, byte, 1), 1, 254)
    scaled = (w * np.exp2(127.0 - byte)[:, None, :]).reshape(k, n).astype(np.float32)
    by_word = np.ascontiguousarray(scaled.reshape(k // 512, 128, 4, n).transpose(0, 1, 3, 2))
    if fmt == "e4m3":
        words = by_word.astype(ml_dtypes.float8_e4m3fn).view(np.uint8)
    else:
        c = by_word.astype(ml_dtypes.float4_e2m1fn).view(np.uint8) & 0xF
        words = c[..., 0::2] | (c[..., 1::2] << 4)
    return np.ascontiguousarray(words), np.ascontiguousarray(byte.astype(np.uint8).reshape(k // 512, 16, n))


def unpack_weight(words, scales, fmt):
    g, p, n, _ = words.shape
    if fmt == "e4m3":
        vals = np.ascontiguousarray(words).view(ml_dtypes.float8_e4m3fn).astype(np.float64)
    else:
        nib = np.empty((g, p, n, 4), np.uint8)
        nib[..., 0::2] = words & 0xF
        nib[..., 1::2] = words >> 4
        vals = E2M1[nib]
    vals = vals * np.repeat(np.exp2(scales.astype(np.float64) - 127.0), 8, axis=1)[..., None]
    return vals.transpose(0, 1, 3, 2).reshape(g * 512, n)


MB, C, H, W, CO, PL, K1, G2, G3, G4, F1, F2, F3 = 16, 1024, 8, 4, 32, 2, 512, 128, 512, 512, 256, 256, 128
HW = H * W


def draw0():
    s, t = mx_kscale(C), mx_kscale(K1)
    x = bf(np.random.standard_normal((MB, C, HW)) * s[None, :, None])
    g1_w = np.random.standard_normal((K1, 2 * C)) * 0.7 / np.sqrt(C) / np.concatenate([s, s])[None, :] * t[:, None]
    g1_w_words, g1_w_scales = pack_weight(g1_w.T, "e4m3")
    g1_b = bf(np.random.standard_normal(K1) * 0.2 * t)
    g2_w = np.random.standard_normal((G2, K1)) * 1.4 / np.sqrt(K1) / t[None, :]
    g2_w_words, g2_w_scales = pack_weight(g2_w.T, "e4m3")
    g2_b = bf(np.random.standard_normal(G2) * 0.2)
    return {"x": x,
            "g1_w_words": g1_w_words,
            "g1_w_scales": g1_w_scales,
            "g1_b": g1_b,
            "g2_w_words": g2_w_words,
            "g2_w_scales": g2_w_scales,
            "g2_b": g2_b}


def core(x, g1_w_words, g1_w_scales, g1_b, g2_w_words, g2_w_scales, g2_b):
    xf = f64(x).transpose(0, 2, 1)
    xq = mxq(xf, 2, "e4m3")
    w1 = unpack_weight(g1_w_words, g1_w_scales, "e4m3").T
    u = xq @ w1[:, :C].T
    v = xq @ w1[:, C:].T
    h = np.maximum(u[:, None, :, :] + v[:, :, None, :] + f64(g1_b), 0.0)
    return np.maximum((mxq(h, 3, "e4m3") @ unpack_weight(g2_w_words, g2_w_scales, "e4m3")) + f64(g2_b), 0.0)


def e4m3fn_bytes(y):
    return np.clip(np.asarray(y, np.float64), -448.0, 448.0).astype(np.float32).astype(ml_dtypes.float8_e4m3fn).view(np.uint8)


def e4m3fn_values(b):
    return np.asarray(b, np.uint8).view(ml_dtypes.float8_e4m3fn).astype(np.float64)


def setup_inputs():
    d = draw0()
    x0 = np.asarray(d['x']).astype(np.float64)
    s = (np.max(np.abs(x0), axis=(0, 2), keepdims=True) / 448.0).astype(np.float32)
    out = {}
    for k, v in d.items():
        if k == 'x':
            out['x_bytes'] = e4m3fn_bytes(x0 / s.astype(np.float64))
            out['x_scale'] = s
        else:
            out[k] = v
    return out


def reference(x_bytes, x_scale, g1_w_words, g1_w_scales, g1_b, g2_w_words, g2_w_scales, g2_b):
    return core(e4m3fn_values(x_bytes) * x_scale.astype(np.float64), g1_w_words, g1_w_scales, g1_b, g2_w_words, g2_w_scales, g2_b)

@@ -1,0 +1,388 @@
+from contextlib import ExitStack
+
+import concourse.mybir as mybir
+from concourse.masks import make_identity
+
+F32 = mybir.dt.float32
+BF16 = mybir.dt.bfloat16
+U32 = mybir.dt.uint32
+I32 = mybir.dt.int32
+U8 = mybir.dt.uint8
+FP8 = mybir.dt.float8_e4m3fn
+FP8X4 = mybir.dt.float8_e4m3fn_x4
+ADD = mybir.AluOpType.add
+MULT = mybir.AluOpType.mult
+RELU = mybir.ActivationFunctionType.Relu
+
+MB, C, HW, K1, G2 = 16, 1024, 32, 512, 128
+P = 128
+T = 4
+FLOPS = 2 * MB * HW * C * K1 * 2 + 2 * MB * HW * HW * K1 * G2
+
+NS = 0
+X_ORDER = [0,"s","w",3,1,2]
+
+V_SAMPLES = [0, 1, 2, 4, 5, 6, 8, 9, 10, 12]
+G_HALVES = [(3, 0), (3, 1), (7, 0), (7, 1), (11, 0), (11, 1), (13, 0), (13, 1), (12, 1)]
+H_SAMPLES = [14, 15]
+USB = {3: 0, 7: 1, 11: 2, 12: 3, 13: 4}
+
+
+def tile_reidrnself_pa_t_w8_kernel(tc, x_bytes, x_scale, g1_w_words, g1_w_scales, g1_b, g2_w_words, g2_w_scales, g2_b, out):
+    nc = tc.nc
+    with ExitStack() as ctx:
+        keep = ctx.enter_context(tc.tile_pool(name="keep", bufs=1))
+        ring = ctx.enter_context(tc.tile_pool(name="ring", bufs=4))
+        psum = ctx.enter_context(tc.psum_pool(name="psum", bufs=1))
+
+        ident = keep.tile([P, P], F32, name="ident")
+        make_identity(nc, ident[:])
+
+        xb = [keep.tile([P, 2 * 4 * P], U8, name="xb%d" % j) for j in range(4)]
+        xw = [keep.tile([P, 2 * 4 * P], BF16, name="xw%d" % j) for j in range(4)]
+        xg = [keep.tile([P, 2 * P * T], BF16, name="xg%d" % j, align_bytes=64) for j in range(4)]
+        xc = [keep.tile([P, 2 * P], U32, name="xc%d" % j, align_bytes=64) for j in range(4)]
+        xs = [keep.tile([P, 2 * P], U8, name="xs%d" % j, align_bytes=64) for j in range(4)]
+        xch = keep.tile([P, 2 * P], U32, name="xch", align_bytes=64)
+        xsh = keep.tile([P, 2 * P], U8, name="xsh", align_bytes=64)
+        scale = keep.tile([P, 2, T], F32, name="scale")
+        b1 = keep.tile([P, T], BF16, name="b1")
+        b1row = keep.tile([P, K1], BF16, name="b1row")
+        b2 = keep.tile([P, 1], BF16, name="b2")
+        w1 = [keep.tile([P, K1], U32, name="w1raw%d" % g) for g in range(4)]
+        w1p = [keep.tile([P, K1], U32, name="w1p%d" % g, align_bytes=64) for g in range(4)]
+        w1s = keep.tile([P, K1], U8, name="w1s")
+        w1sp = keep.tile([P, K1], U8, name="w1sp", align_bytes=64)
+        w2 = keep.tile([P, G2], U32, name="w2", align_bytes=64)
+        w2s = keep.tile([P, G2], U8, name="w2s", align_bytes=64)
+        vb = keep.tile([P, MB * HW, T], F32, name="vb", align_bytes=64)
+        usb = [keep.tile([P, HW, T], F32, name="usb%d" % i, align_bytes=64) for i in range(5)]
+        uv = keep.tile([P, K1], F32, name="uv")
+        sel = [keep.tile([P, HW * HW], F32, name="sel%d" % i) for i in range(2)]
+        pre = [keep.tile([P, HW * HW * T], BF16, name="pre%d" % i, align_bytes=64) for i in range(3)]
+        hv = [keep.tile([P, HW * HW * T], BF16, name="hv%d" % i, align_bytes=64) for i in range(2)]
+        hg = [keep.tile([P, HW * HW * T // 2], BF16, name="hg%d" % i, align_bytes=64) for i in range(2)]
+        hh = [keep.tile([P, HW * HW * T // 2], BF16, name="hh%d" % i, align_bytes=64) for i in range(2)]
+        cv = [keep.tile([P, HW * HW], U32, name="cv%d" % i, align_bytes=64) for i in range(2)]
+        sv = [keep.tile([P, HW * HW], U8, name="sv%d" % i, align_bytes=64) for i in range(2)]
+        cg = [keep.tile([P, HW * HW // 2], U32, name="cg%d" % i, align_bytes=64) for i in range(2)]
+        sg = [keep.tile([P, HW * HW // 2], U8, name="sg%d" % i, align_bytes=64) for i in range(2)]
+        ch = [keep.tile([P, HW * HW // 2], U32, name="ch%d" % i, align_bytes=64) for i in range(2)]
+        sh = [keep.tile([P, HW * HW // 2], U8, name="sh%d" % i, align_bytes=64) for i in range(2)]
+        warm = keep.tile([P, 1], F32, name="warm")
+        warm2 = keep.tile([P, 1], F32, name="warm2")
+
+        ubank = {}
+        state = {"y": 0, "tmp": 0}
+
+        def tmp_bank(name):
+            n = state["tmp"]
+            state["tmp"] = n + 1
+            return psum.tile([P, 512], F32, name="%s%d" % (name, n), tag="tmp", bufs=3)
+
+        def load_x(j):
+            for g in range(2):
+                nc.sync.dma_start(
+                    out=xb[j][:, g * 512:(g + 1) * 512].rearrange("q (b n) -> q b n", b=4),
+                    in_=x_bytes[4 * j:4 * j + 4, g * 512:(g + 1) * 512, :].rearrange("b (q t) n -> q b (t n)", t=T),
+                )
+
+        def cast_x(j):
+            nc.scalar.copy(out=xw[j][:], in_=xb[j][:].bitcast(FP8))
+
+        def mul_x(j):
+            for g in range(2):
+                nc.vector.tensor_tensor(
+                    out=xg[j][:, g * 512:(g + 1) * 512].rearrange("q (b n t) -> q b n t", b=4, t=T),
+                    in0=xw[j][:, g * 512:(g + 1) * 512].rearrange("q (b t n) -> q b n t", b=4, t=T),
+                    in1=scale[:, g, :].unsqueeze(1).unsqueeze(1).broadcast_to([P, 4, HW, T]),
+                    op=MULT,
+                )
+            nc.vector.quantize_mx(out=xc[j][:].bitcast(FP8X4), scales=xs[j][:], in_=xg[j][:])
+
+        def dup_h():
+            for k in range(2):
+                nc.vector.tensor_copy(
+                    out=xch[:].bitcast(I32).rearrange("q (g n) -> q g n", g=2)[:, :, 64 * k:64 * k + 64],
+                    in_=xc[3][:].bitcast(I32).rearrange("q (g n) -> q g n", g=2)[:, :, 64:128],
+                )
+                nc.vector.tensor_copy(
+                    out=xsh[:].rearrange("q (g n) -> q g n", g=2)[:, :, 64 * k:64 * k + 64],
+                    in_=xs[3][:].rearrange("q (g n) -> q g n", g=2)[:, :, 64:128],
+                )
+
+        def stage1(j, bank, first_group):
+            for t in range(T):
+                for g in range(2):
+                    w = first_group + g
+                    nc.tensor.matmul_mx(
+                        out=bank[:, t * P:(t + 1) * P],
+                        lhsT=w1p[w][:, t * P:(t + 1) * P].bitcast(FP8X4),
+                        lhsT_scale=w1sp[4 * w:P, t * P:(t + 1) * P],
+                        rhs=xc[j][:, g * P:(g + 1) * P].bitcast(FP8X4),
+                        rhs_scale=xs[j][:, g * P:(g + 1) * P],
+                        start=(g == 0),
+                        stop=(g == 1),
+                    )
+
+        def stage1_h(bank, first_group):
+            for g in range(2):
+                w = first_group + g
+                nc.tensor.matmul_mx(
+                    out=bank[:],
+                    lhsT=xch[:, g * P:(g + 1) * P].bitcast(FP8X4),
+                    lhsT_scale=xsh[:, g * P:(g + 1) * P],
+                    rhs=w1p[w][:].bitcast(FP8X4),
+                    rhs_scale=w1sp[4 * w:P, :],
+                    start=(g == 0),
+                    stop=(g == 1),
+                )
+
+        def u_view(s):
+            return ubank[s // 4][:].rearrange("q (t r) -> q r t", t=T)[:, 32 * (s % 4):32 * (s % 4) + 32, :]
+
+        def make_u(j):
+            if j < 3:
+                ubank[j] = psum.tile([P, 512], F32, name="u_of_%d" % j, tag="ubank%d" % j)
+            else:
+                ubank[j] = tmp_bank("u_of_3_")
+            stage1(j, ubank[j], 0)
+            for smp in USB:
+                if smp // 4 == j:
+                    nc.scalar.copy(out=usb[USB[smp]][:], in_=u_view(smp))
+
+        vbank = {}
+
+        def make_v(j):
+            vbank[j] = tmp_bank("v_of_%d_" % j)
+            stage1(j, vbank[j], 2)
+
+        def bias_v(j):
+            nc.vector.tensor_tensor(
+                out=vb[:, j * P:(j + 1) * P, :],
+                in0=vbank[j][:].rearrange("q (t r) -> q r t", t=T),
+                in1=b1[:].unsqueeze(1).broadcast_to([P, P, T]),
+                op=ADD,
+            )
+
+        def make_uv_h():
+            bank = tmp_bank("uh")
+            stage1_h(bank, 0)
+            nc.scalar.copy(out=uv[0:64, :], in_=bank[0:64, :])
+            vbank["h"] = tmp_bank("vh")
+            stage1_h(vbank["h"], 2)
+
+        def bias_v_h():
+            nc.vector.tensor_tensor(
+                out=uv[64:128, :].rearrange("q (t m) -> q t m", t=T),
+                in0=vbank["h"][64:128, :].rearrange("q (t m) -> q t m", t=T),
+                in1=b1row[64:128, :].rearrange("q (m t) -> q t m", t=T),
+                op=ADD,
+            )
+
+        def make_sel(i):
+            nc.gpsimd.tensor_tensor(
+                out=sel[i][:].rearrange("q (a p) -> q a p", p=HW),
+                in0=ident[:, 32 * i:32 * i + 32].unsqueeze(1).broadcast_to([P, HW, HW]),
+                in1=ident[:, 64 + 32 * i:64 + 32 * i + 32].unsqueeze(2).broadcast_to([P, HW, HW]),
+                op=ADD,
+            )
+
+        def add_v(c, a0, a1):
+            s = V_SAMPLES[c]
+            n = a1 - a0
+            u = usb[USB[s]][:] if s in USB else u_view(s)
+            nc.vector.tensor_tensor(
+                out=pre[c % 3][:, a0 * P:a1 * P].rearrange("q (a p t) -> q a p t", p=HW, t=T),
+                in0=u.unsqueeze(1).broadcast_to([P, n, HW, T]),
+                in1=vb[:, 32 * s + a0:32 * s + a1, :].unsqueeze(2).broadcast_to([P, n, HW, T]),
+                op=ADD,
+            )
+
+        def add_g(c):
+            s, half = G_HALVES[c]
+            a0 = 32 * s + 16 * half
+            nc.gpsimd.tensor_tensor(
+                out=pre[(c + 2) % 3][:, 0:16 * P].rearrange("q (a p t) -> q a p t", p=HW, t=T),
+                in0=usb[USB[s]][:].unsqueeze(1).broadcast_to([P, 16, HW, T]),
+                in1=vb[:, a0:a0 + 16, :].unsqueeze(2).broadcast_to([P, 16, HW, T]),
+                op=ADD,
+            )
+
+        def relu_v(c, a0, a1):
+            nc.vector.tensor_scalar_max(hv[c % 2][:, a0 * P:a1 * P], pre[c % 3][:, a0 * P:a1 * P], 0.0)
+
+        def relu_s(c, a0, a1):
+            nc.scalar.activation(out=hv[c % 2][:, a0 * P:a1 * P], in_=pre[c % 3][:, a0 * P:a1 * P], func=RELU)
+
+        def relu_g(c):
+            nc.scalar.activation(out=hg[c % 2][:], in_=pre[(c + 2) % 3][:, 0:16 * P], func=RELU)
+
+        def chunk_h(k):
+            i, r = k // 8, k % 8
+            bank = tmp_bank("hc")
+            for t in range(T):
+                nc.tensor.matmul(bank[:, t * P:(t + 1) * P], lhsT=uv[:, t * P:(t + 1) * P], rhs=sel[i][:, r * P:(r + 1) * P], start=True, stop=True)
+            return bank
+
+        def relu_h(k, bank):
+            r = k % 4
+            nc.scalar.activation(
+                out=hh[(k // 4) % 2][:, r * 512:(r + 1) * 512].rearrange("q (n t) -> q n t", t=T),
+                in_=bank[:].rearrange("q (t n) -> q n t", t=T),
+                func=RELU,
+            )
+
+        def quant_v(c, p0, p1):
+            nc.vector.quantize_mx(out=cv[c % 2][:, p0:p1].bitcast(FP8X4), scales=sv[c % 2][:, p0:p1], in_=hv[c % 2][:, p0 * T:p1 * T])
+
+        def quant_half(codes, scales, h):
+            nc.vector.quantize_mx(out=codes[:].bitcast(FP8X4), scales=scales[:], in_=h[:])
+
+        def mm(u):
+            n = state["y"]
+            state["y"] = n + 1
+            y = psum.tile([P, 512], F32, name="y%d" % n, tag="ybank%d" % (n % 2))
+            nc.tensor.matmul_mx(out=y[:], lhsT=w2[:].bitcast(FP8X4), lhsT_scale=w2s[:], rhs=u["codes"].bitcast(FP8X4), rhs_scale=u["scales"], start=True, stop=True)
+            u["y"] = y
+
+        def pass1(u):
+            ys = ring.tile([P, 512], F32, name="ys")
+            nc.scalar.activation(out=ys[:], in_=u["y"][:], func=RELU, bias=b2[:, 0:1])
+            u["ys"] = ys
+
+        def turn(u):
+            tb = tmp_bank("tr")
+            for j in range(4):
+                nc.tensor.transpose(tb[:, j * P:(j + 1) * P], u["ys"][:, j * P:(j + 1) * P], ident[:])
+            u["t"] = tb
+
+        def pass2(u, on_vector=False):
+            o = ring.tile([P, 4, P], F32, name="o")
+            if on_vector:
+                nc.vector.tensor_copy(out=o[:], in_=u["t"][:].rearrange("q (j c) -> q j c", j=4))
+            else:
+                nc.scalar.copy(out=o[:], in_=u["t"][:].rearrange("q (j c) -> q j c", j=4))
+            half = u["half"]
+            rows = out[u["s"]].rearrange("a p c -> (a p) c")[half * 512:(half + 1) * 512, :]
+            nc.sync.dma_start(out=rows.rearrange("(j q) c -> q j c", q=P), in_=o[:])
+
+        def epilogue(units, hq, tail):
+            n = len(units)
+            banks = [None, None]
+            if hq:
+                banks[0] = chunk_h(hq[0])
+            for u in units[:2]:
+                mm(u)
+            for u in units[:2]:
+                pass1(u)
+            if hq:
+                relu_h(hq[0], banks[0])
+            for i in range(n):
+                turn(units[i])
+                if i + 2 < n:
+                    mm(units[i + 2])
+                if i == 0 and hq:
+                    banks[1] = chunk_h(hq[1])
+                pass2(units[i], tail and i % 2 == 0)
+                if i + 2 < n:
+                    pass1(units[i + 2])
+                if i == min(1, n - 1) and hq:
+                    relu_h(hq[1], banks[1])
+            if n == 0 and hq:
+                banks[1] = chunk_h(hq[1])
+                relu_h(hq[1], banks[1])
+
+        with tc.manual_schedule():
+            nc.scalar.dma_start(out=scale[:], in_=x_scale.rearrange("o (g q t) z -> q (o g) (t z)", q=P, t=T))
+            nc.scalar.dma_start(out=b1[:], in_=g1_b.rearrange("(q t) -> q t", t=T))
+            nc.scalar.dma_start(out=b2[:], in_=g2_b.rearrange("(q o) -> q o", o=1))
+            nc.scalar.dma_start(out=b1row[:], in_=g1_b.partition_broadcast(P))
+            nc.vector.memset(warm[:], 0.0)
+            nc.vector.memset(w1s[:].bitcast(I32), 0)
+            nc.vector.memset(w2s[:].bitcast(I32), 0)
+            nc.scalar.activation(out=warm2[:], in_=warm[:], func=RELU)
+            make_sel(0)
+            make_sel(1)
+            for item in X_ORDER:
+                if item == "s":
+                    for q in range(4):
+                        nc.sync.dma_start(out=w1s[32 * q:32 * q + 16, :].bitcast(I32), in_=g1_w_scales[:, 4 * q:4 * q + 4, :].bitcast(I32))
+                elif item == "w":
+                    for g in range(4):
+                        nc.sync.dma_start(out=w1[g][:].bitcast(I32), in_=g1_w_words[g].rearrange("q n t -> q (n t)").bitcast(I32))
+                else:
+                    load_x(item)
+            nc.sync.dma_start(out=w2[:].bitcast(I32), in_=g2_w_words[0].rearrange("q n t -> q (n t)").bitcast(I32))
+            for q in range(4):
+                nc.sync.dma_start(out=w2s[32 * q:32 * q + 4, :].bitcast(I32), in_=g2_w_scales[0, 4 * q:4 * q + 4, :].bitcast(I32))
+
+            cast_x(0)
+            mul_x(0)
+            nc.vector.tensor_copy(out=w1sp[:].rearrange("q (t m) -> q t m", t=T), in_=w1s[:].rearrange("q (m t) -> q t m", t=T))
+            for g in range(4):
+                nc.vector.tensor_copy(
+                    out=w1p[g][:].bitcast(I32).rearrange("q (t m) -> q t m", t=T),
+                    in_=w1[g][:].bitcast(I32).rearrange("q (m t) -> q t m", t=T),
+                )
+            make_u(0)
+            make_v(0)
+            bias_v(0)
+            cast_x(3)
+            cast_x(1)
+            cast_x(2)
+
+            last = len(V_SAMPLES) - 1
+            n_g = len(G_HALVES)
+            h_ready = []
+            for c in range(last + 2):
+                units = []
+                if c <= last:
+                    add_v(c, 0, 32 if c < last else 16)
+                if c < n_g:
+                    add_g(c)
+                if c == 0:
+                    mul_x(3)
+                    dup_h()
+                    mul_x(1)
+                    make_u(3)
+                    make_v(3)
+                    bias_v(3)
+                    make_uv_h()
+                    bias_v_h()
+                    make_u(1)
+                    make_v(1)
+                elif c == 1:
+                    mul_x(2)
+                    bias_v(1)
+                    make_u(2)
+                    make_v(2)
+                elif c == 2:
+                    bias_v(2)
+                if c >= 1:
+                    k = c - 1
+                    pairs = 1024 if k < last else 512
+                    quant_v(k, 0, pairs)
+                    for half in range(pairs // 512):
+                        units.append({"codes": cv[k % 2][:, half * 512:(half + 1) * 512], "scales": sv[k % 2][:, half * 512:(half + 1) * 512], "s": V_SAMPLES[k], "half": half})
+                    if k < n_g:
+                        quant_half(cg[k % 2], sg[k % 2], hg[k % 2])
+                        units.append({"codes": cg[k % 2][:], "scales": sg[k % 2][:], "s": G_HALVES[k][0], "half": G_HALVES[k][1]})
+                for n in h_ready:
+                    quant_half(ch[n % 2], sh[n % 2], hh[n % 2])
+                    units.append({"codes": ch[n % 2][:], "scales": sh[n % 2][:], "s": H_SAMPLES[n // 2], "half": n % 2})
+                h_ready = []
+                if c < last:
+                    relu_v(c, 0, 32 - NS)
+                elif c == last:
+                    relu_v(c, 0, 16)
+                if c < n_g:
+                    relu_g(c)
+                if c < last and NS:
+                    relu_s(c, 32 - NS, 32)
+                hq = []
+                if 1 <= c <= 8:
+                    hq = [2 * (c - 1), 2 * (c - 1) + 1]
+                    if hq[1] % 4 == 3:
+                        h_ready = [hq[1] // 4]
+                epilogue(units, hq, c >= last)

@@ -12,6 +12,8 @@ FP8 = mybir.dt.float8_e4m3fn
 FP8X4 = mybir.dt.float8_e4m3fn_x4
 ADD = mybir.AluOpType.add
 MULT = mybir.AluOpType.mult
+MAX = mybir.AluOpType.max
+COPY = mybir.ActivationFunctionType.Copy
 RELU = mybir.ActivationFunctionType.Relu
 
 MB, C, HW, K1, G2 = 16, 1024, 32, 512, 128
@@ -19,12 +21,13 @@ P = 128
 T = 4
 FLOPS = 2 * MB * HW * C * K1 * 2 + 2 * MB * HW * HW * K1 * G2
 
-NS = 0
+H_CHUNKS = [3, 3, 2, 2, 2, 2, 2, 0, 0]
 X_ORDER = [0,"s","w",3,1,2]
 
 V_SAMPLES = [0, 1, 2, 4, 5, 6, 8, 9, 10, 12]
 G_HALVES = [(3, 0), (3, 1), (7, 0), (7, 1), (11, 0), (11, 1), (13, 0), (13, 1), (12, 1)]
 H_SAMPLES = [14, 15]
+TAIL_TAGS = ["ybank0", "ybank1", "ubank0", "ubank1", "ubank2"]
 USB = {3: 0, 7: 1, 11: 2, 12: 3, 13: 4}
 
 
@@ -55,7 +58,7 @@ def tile_reidrnself_pa_t_w8_kernel(tc, x_bytes, x_scale, g1_w_words, g1_w_scales
         w1sp = keep.tile([P, K1], U8, name="w1sp", align_bytes=64)
         w2 = keep.tile([P, G2], U32, name="w2", align_bytes=64)
         w2s = keep.tile([P, G2], U8, name="w2s", align_bytes=64)
-        vb = keep.tile([P, MB * HW, T], F32, name="vb", align_bytes=64)
+        vb = keep.tile([P, 448, T], F32, name="vb", align_bytes=64)
         usb = [keep.tile([P, HW, T], F32, name="usb%d" % i, align_bytes=64) for i in range(5)]
         uv = keep.tile([P, K1], F32, name="uv")
         sel = [keep.tile([P, HW * HW], F32, name="sel%d" % i) for i in range(2)]
@@ -69,6 +72,7 @@ def tile_reidrnself_pa_t_w8_kernel(tc, x_bytes, x_scale, g1_w_words, g1_w_scales
         sg = [keep.tile([P, HW * HW // 2], U8, name="sg%d" % i, align_bytes=64) for i in range(2)]
         ch = [keep.tile([P, HW * HW // 2], U32, name="ch%d" % i, align_bytes=64) for i in range(2)]
         sh = [keep.tile([P, HW * HW // 2], U8, name="sh%d" % i, align_bytes=64) for i in range(2)]
+        b2f = keep.tile([P, 1], F32, name="b2f")
         warm = keep.tile([P, 1], F32, name="warm")
         warm2 = keep.tile([P, 1], F32, name="warm2")
 
@@ -90,6 +94,19 @@ def tile_reidrnself_pa_t_w8_kernel(tc, x_bytes, x_scale, g1_w_words, g1_w_scales
         def cast_x(j):
             nc.scalar.copy(out=xw[j][:], in_=xb[j][:].bitcast(FP8))
 
+        def scale_on_scalar(j):
+            for g in range(2):
+                for t in range(T):
+                    nc.scalar.activation(
+                        out=xg[j][:, g * 512:(g + 1) * 512].rearrange("q (b n t) -> q t b n", b=4, t=T)[:, t, :, :],
+                        in_=xw[j][:, g * 512:(g + 1) * 512].rearrange("q (b t n) -> q t b n", b=4, t=T)[:, t, :, :],
+                        func=COPY,
+                        scale=scale[:, g, t:t + 1],
+                    )
+
+        def cast_on_vector(j):
+            nc.vector.tensor_copy(out=xw[j][:], in_=xb[j][:].bitcast(FP8))
+
         def mul_x(j):
             for g in range(2):
                 nc.vector.tensor_tensor(
@@ -98,6 +115,8 @@ def tile_reidrnself_pa_t_w8_kernel(tc, x_bytes, x_scale, g1_w_words, g1_w_scales
                     in1=scale[:, g, :].unsqueeze(1).unsqueeze(1).broadcast_to([P, 4, HW, T]),
                     op=MULT,
                 )
+
+        def quant_x(j):
             nc.vector.quantize_mx(out=xc[j][:].bitcast(FP8X4), scales=xs[j][:], in_=xg[j][:])
 
         def dup_h():
@@ -158,10 +177,11 @@ def tile_reidrnself_pa_t_w8_kernel(tc, x_bytes, x_scale, g1_w_words, g1_w_scales
             stage1(j, vbank[j], 2)
 
         def bias_v(j):
+            n = P if j < 3 else 64
             nc.vector.tensor_tensor(
-                out=vb[:, j * P:(j + 1) * P, :],
-                in0=vbank[j][:].rearrange("q (t r) -> q r t", t=T),
-                in1=b1[:].unsqueeze(1).broadcast_to([P, P, T]),
+                out=vb[:, j * P:j * P + n, :],
+                in0=vbank[j][:].rearrange("q (t r) -> q r t", t=T)[:, 0:n, :],
+                in1=b1[:].unsqueeze(1).broadcast_to([P, n, T]),
                 op=ADD,
             )
 
@@ -180,12 +200,24 @@ def tile_reidrnself_pa_t_w8_kernel(tc, x_bytes, x_scale, g1_w_words, g1_w_scales
                 op=ADD,
             )
 
-        def make_sel(i):
+        def make_sel_g(i):
             nc.gpsimd.tensor_tensor(
                 out=sel[i][:].rearrange("q (a p) -> q a p", p=HW),
                 in0=ident[:, 32 * i:32 * i + 32].unsqueeze(1).broadcast_to([P, HW, HW]),
                 in1=ident[:, 64 + 32 * i:64 + 32 * i + 32].unsqueeze(2).broadcast_to([P, HW, HW]),
                 op=ADD,
+            )
+
+        def make_sel_s(i):
+            r0 = 32 * i
+            r1 = 64 + 32 * i
+            nc.scalar.copy(
+                out=sel[i][r0:r0 + 32, :].rearrange("q (a p) -> q a p", p=HW),
+                in_=ident[r0:r0 + 32, r0:r0 + 32].unsqueeze(1).broadcast_to([32, HW, HW]),
+            )
+            nc.scalar.copy(
+                out=sel[i][r1:r1 + 32, :].rearrange("q (a p) -> q a p", p=HW),
+                in_=ident[r1:r1 + 32, r1:r1 + 32].unsqueeze(2).broadcast_to([32, HW, HW]),
             )
 
         def add_v(c, a0, a1):
@@ -212,9 +244,6 @@ def tile_reidrnself_pa_t_w8_kernel(tc, x_bytes, x_scale, g1_w_words, g1_w_scales
         def relu_v(c, a0, a1):
             nc.vector.tensor_scalar_max(hv[c % 2][:, a0 * P:a1 * P], pre[c % 3][:, a0 * P:a1 * P], 0.0)
 
-        def relu_s(c, a0, a1):
-            nc.scalar.activation(out=hv[c % 2][:, a0 * P:a1 * P], in_=pre[c % 3][:, a0 * P:a1 * P], func=RELU)
-
         def relu_g(c):
             nc.scalar.activation(out=hg[c % 2][:], in_=pre[(c + 2) % 3][:, 0:16 * P], func=RELU)
 
@@ -239,17 +268,20 @@ def tile_reidrnself_pa_t_w8_kernel(tc, x_bytes, x_scale, g1_w_words, g1_w_scales
         def quant_half(codes, scales, h):
             nc.vector.quantize_mx(out=codes[:].bitcast(FP8X4), scales=scales[:], in_=h[:])
 
-        def mm(u):
+        def mm(u, tag=None):
             n = state["y"]
             state["y"] = n + 1
-            y = psum.tile([P, 512], F32, name="y%d" % n, tag="ybank%d" % (n % 2))
+            y = psum.tile([P, 512], F32, name="y%d" % n, tag=tag or "ybank%d" % (n % 2))
             nc.tensor.matmul_mx(out=y[:], lhsT=w2[:].bitcast(FP8X4), lhsT_scale=w2s[:], rhs=u["codes"].bitcast(FP8X4), rhs_scale=u["scales"], start=True, stop=True)
             u["y"] = y
 
-        def pass1(u):
+        def pass1(u, on_vector=False):
             ys = ring.tile([P, 512], F32, name="ys")
-            nc.scalar.activation(out=ys[:], in_=u["y"][:], func=RELU, bias=b2[:, 0:1])
             u["ys"] = ys
+            if on_vector:
+                nc.vector.tensor_scalar(out=ys[:], in0=u["y"][:], scalar1=b2f[:, 0:1], scalar2=0.0, op0=ADD, op1=MAX)
+                return
+            nc.scalar.activation(out=ys[:], in_=u["y"][:], func=RELU, bias=b2[:, 0:1])
 
         def turn(u):
             tb = tmp_bank("tr")
@@ -267,31 +299,21 @@ def tile_reidrnself_pa_t_w8_kernel(tc, x_bytes, x_scale, g1_w_words, g1_w_scales
             rows = out[u["s"]].rearrange("a p c -> (a p) c")[half * 512:(half + 1) * 512, :]
             nc.sync.dma_start(out=rows.rearrange("(j q) c -> q j c", q=P), in_=o[:])
 
-        def epilogue(units, hq, tail):
+        def epilogue(units, hq):
             n = len(units)
-            banks = [None, None]
-            if hq:
-                banks[0] = chunk_h(hq[0])
+            for k, bank in [(k, chunk_h(k)) for k in hq]:
+                relu_h(k, bank)
             for u in units[:2]:
                 mm(u)
             for u in units[:2]:
                 pass1(u)
-            if hq:
-                relu_h(hq[0], banks[0])
             for i in range(n):
                 turn(units[i])
                 if i + 2 < n:
                     mm(units[i + 2])
-                if i == 0 and hq:
-                    banks[1] = chunk_h(hq[1])
-                pass2(units[i], tail and i % 2 == 0)
+                pass2(units[i])
                 if i + 2 < n:
                     pass1(units[i + 2])
-                if i == min(1, n - 1) and hq:
-                    relu_h(hq[1], banks[1])
-            if n == 0 and hq:
-                banks[1] = chunk_h(hq[1])
-                relu_h(hq[1], banks[1])
 
         with tc.manual_schedule():
             nc.scalar.dma_start(out=scale[:], in_=x_scale.rearrange("o (g q t) z -> q (o g) (t z)", q=P, t=T))
@@ -302,14 +324,15 @@ def tile_reidrnself_pa_t_w8_kernel(tc, x_bytes, x_scale, g1_w_words, g1_w_scales
             nc.vector.memset(w1s[:].bitcast(I32), 0)
             nc.vector.memset(w2s[:].bitcast(I32), 0)
             nc.scalar.activation(out=warm2[:], in_=warm[:], func=RELU)
-            make_sel(0)
-            make_sel(1)
+            nc.vector.memset(sel[1][:], 0.0)
+            make_sel_g(0)
+            make_sel_s(1)
             for item in X_ORDER:
                 if item == "s":
                     for q in range(4):
                         nc.sync.dma_start(out=w1s[32 * q:32 * q + 16, :].bitcast(I32), in_=g1_w_scales[:, 4 * q:4 * q + 4, :].bitcast(I32))
                 elif item == "w":
-                    for g in range(4):
+                    for g in (2, 3, 0, 1):
                         nc.sync.dma_start(out=w1[g][:].bitcast(I32), in_=g1_w_words[g].rearrange("q n t -> q (n t)").bitcast(I32))
                 else:
                     load_x(item)
@@ -317,72 +340,93 @@ def tile_reidrnself_pa_t_w8_kernel(tc, x_bytes, x_scale, g1_w_words, g1_w_scales
             for q in range(4):
                 nc.sync.dma_start(out=w2s[32 * q:32 * q + 4, :].bitcast(I32), in_=g2_w_scales[0, 4 * q:4 * q + 4, :].bitcast(I32))
 
-            cast_x(0)
+            cast_on_vector(0)
+            nc.vector.tensor_copy(out=b2f[:], in_=b2[:])
             mul_x(0)
+            quant_x(0)
             nc.vector.tensor_copy(out=w1sp[:].rearrange("q (t m) -> q t m", t=T), in_=w1s[:].rearrange("q (m t) -> q t m", t=T))
-            for g in range(4):
+            for g in (2, 3, 0, 1):
                 nc.vector.tensor_copy(
                     out=w1p[g][:].bitcast(I32).rearrange("q (t m) -> q t m", t=T),
                     in_=w1[g][:].bitcast(I32).rearrange("q (m t) -> q t m", t=T),
                 )
-            make_u(0)
+            cast_x(3)
             make_v(0)
             bias_v(0)
-            cast_x(3)
+            make_u(0)
+            scale_on_scalar(3)
             cast_x(1)
             cast_x(2)
 
             last = len(V_SAMPLES) - 1
             n_g = len(G_HALVES)
             h_ready = []
-            for c in range(last + 2):
+            for c in range(last):
                 units = []
-                if c <= last:
-                    add_v(c, 0, 32 if c < last else 16)
+                add_v(c, 0, 32)
                 if c < n_g:
                     add_g(c)
                 if c == 0:
-                    mul_x(3)
+                    quant_x(3)
                     dup_h()
-                    mul_x(1)
                     make_u(3)
                     make_v(3)
-                    bias_v(3)
-                    make_uv_h()
-                    bias_v_h()
-                    make_u(1)
-                    make_v(1)
                 elif c == 1:
-                    mul_x(2)
-                    bias_v(1)
-                    make_u(2)
-                    make_v(2)
+                    quant_x(1)
                 elif c == 2:
-                    bias_v(2)
+                    mul_x(2)
+                    quant_x(2)
                 if c >= 1:
                     k = c - 1
-                    pairs = 1024 if k < last else 512
-                    quant_v(k, 0, pairs)
-                    for half in range(pairs // 512):
+                    quant_v(k, 0, 1024)
+                    for half in range(2):
                         units.append({"codes": cv[k % 2][:, half * 512:(half + 1) * 512], "scales": sv[k % 2][:, half * 512:(half + 1) * 512], "s": V_SAMPLES[k], "half": half})
-                    if k < n_g:
-                        quant_half(cg[k % 2], sg[k % 2], hg[k % 2])
-                        units.append({"codes": cg[k % 2][:], "scales": sg[k % 2][:], "s": G_HALVES[k][0], "half": G_HALVES[k][1]})
+                    quant_half(cg[k % 2], sg[k % 2], hg[k % 2])
+                    units.append({"codes": cg[k % 2][:], "scales": sg[k % 2][:], "s": G_HALVES[k][0], "half": G_HALVES[k][1]})
                 for n in h_ready:
                     quant_half(ch[n % 2], sh[n % 2], hh[n % 2])
                     units.append({"codes": ch[n % 2][:], "scales": sh[n % 2][:], "s": H_SAMPLES[n // 2], "half": n % 2})
                 h_ready = []
-                if c < last:
-                    relu_v(c, 0, 32 - NS)
-                elif c == last:
-                    relu_v(c, 0, 16)
-                if c < n_g:
+                relu_v(c, 0, 32)
+                if c < last - 1:
                     relu_g(c)
-                if c < last and NS:
-                    relu_s(c, 32 - NS, 32)
-                hq = []
-                if 1 <= c <= 8:
-                    hq = [2 * (c - 1), 2 * (c - 1) + 1]
-                    if hq[1] % 4 == 3:
-                        h_ready = [hq[1] // 4]
-                epilogue(units, hq, c >= last)
+                if c == 0:
+                    make_uv_h()
+                    bias_v(3)
+                    bias_v_h()
+                    scale_on_scalar(1)
+                elif c in (1, 2):
+                    make_u(c)
+                    make_v(c)
+                    bias_v(c)
+                done = sum(H_CHUNKS[:c])
+                hq = list(range(done, done + H_CHUNKS[c]))
+                h_ready = [k // 4 for k in hq if k % 4 == 3]
+                epilogue(units, hq)
+
+            k = last - 1
+            add_v(last, 0, 16)
+            quant_v(k, 0, 1024)
+            nc.vector.tensor_scalar_max(hg[k % 2][:], pre[(k + 2) % 3][:, 0:16 * P], 0.0)
+            relu_v(last, 0, 16)
+            quant_half(cg[k % 2], sg[k % 2], hg[k % 2])
+            quant_v(last, 0, 512)
+            tail = [{"codes": cv[k % 2][:, half * 512:(half + 1) * 512], "scales": sv[k % 2][:, half * 512:(half + 1) * 512], "s": V_SAMPLES[k], "half": half} for half in range(2)]
+            tail.append({"codes": cg[k % 2][:], "scales": sg[k % 2][:], "s": G_HALVES[k][0], "half": G_HALVES[k][1]})
+            tail.append({"codes": cv[last % 2][:, 0:512], "scales": sv[last % 2][:, 0:512], "s": V_SAMPLES[last], "half": 0})
+            mm(tail[0], TAIL_TAGS[0])
+            mm(tail[1], TAIL_TAGS[1])
+            pass1(tail[0])
+            pass1(tail[1])
+            turn(tail[0])
+            pass2(tail[0])
+            turn(tail[1])
+            mm(tail[2], TAIL_TAGS[2])
+            pass2(tail[1])
+            mm(tail[3], TAIL_TAGS[3])
+            pass1(tail[2])
+            pass1(tail[3], True)
+            turn(tail[2])
+            turn(tail[3])
+            pass2(tail[2])
+            pass2(tail[3], True)

@@ -21,7 +21,7 @@ P = 128
 T = 4
 FLOPS = 2 * MB * HW * C * K1 * 2 + 2 * MB * HW * HW * K1 * G2
 
-H_CHUNKS = [3, 3, 2, 2, 2, 2, 2, 0, 0]
+H_CHUNKS = [2, 2, 2, 2, 2, 2, 2, 2, 0]
 X_ORDER = [0,"s","w",3,1,2]
 
 V_SAMPLES = [0, 1, 2, 4, 5, 6, 8, 9, 10, 12]
@@ -35,7 +35,7 @@ def tile_reidrnself_pa_t_w8_kernel(tc, x_bytes, x_scale, g1_w_words, g1_w_scales
     nc = tc.nc
     with ExitStack() as ctx:
         keep = ctx.enter_context(tc.tile_pool(name="keep", bufs=1))
-        ring = ctx.enter_context(tc.tile_pool(name="ring", bufs=4))
+        ring = ctx.enter_context(tc.tile_pool(name="ring", bufs=6))
         psum = ctx.enter_context(tc.psum_pool(name="psum", bufs=1))
 
         ident = keep.tile([P, P], F32, name="ident")
@@ -62,7 +62,7 @@ def tile_reidrnself_pa_t_w8_kernel(tc, x_bytes, x_scale, g1_w_words, g1_w_scales
         usb = [keep.tile([P, HW, T], F32, name="usb%d" % i, align_bytes=64) for i in range(5)]
         uv = keep.tile([P, K1], F32, name="uv")
         sel = [keep.tile([P, HW * HW], F32, name="sel%d" % i) for i in range(2)]
-        pre = [keep.tile([P, HW * HW * T], BF16, name="pre%d" % i, align_bytes=64) for i in range(3)]
+        pre = [keep.tile([P, HW * HW * T], BF16, name="pre%d" % i, align_bytes=64) for i in range(2)]
         hv = [keep.tile([P, HW * HW * T], BF16, name="hv%d" % i, align_bytes=64) for i in range(2)]
         hg = [keep.tile([P, HW * HW * T // 2], BF16, name="hg%d" % i, align_bytes=64) for i in range(2)]
         hh = [keep.tile([P, HW * HW * T // 2], BF16, name="hh%d" % i, align_bytes=64) for i in range(2)]
@@ -176,12 +176,11 @@ def tile_reidrnself_pa_t_w8_kernel(tc, x_bytes, x_scale, g1_w_words, g1_w_scales
             vbank[j] = tmp_bank("v_of_%d_" % j)
             stage1(j, vbank[j], 2)
 
-        def bias_v(j):
-            n = P if j < 3 else 64
+        def bias_v(j, r0, r1):
             nc.vector.tensor_tensor(
-                out=vb[:, j * P:j * P + n, :],
-                in0=vbank[j][:].rearrange("q (t r) -> q r t", t=T)[:, 0:n, :],
-                in1=b1[:].unsqueeze(1).broadcast_to([P, n, T]),
+                out=vb[:, j * P + r0:j * P + r1, :],
+                in0=vbank[j][:].rearrange("q (t r) -> q r t", t=T)[:, r0:r1, :],
+                in1=b1[:].unsqueeze(1).broadcast_to([P, r1 - r0, T]),
                 op=ADD,
             )
 
@@ -225,7 +224,7 @@ def tile_reidrnself_pa_t_w8_kernel(tc, x_bytes, x_scale, g1_w_words, g1_w_scales
             n = a1 - a0
             u = usb[USB[s]][:] if s in USB else u_view(s)
             nc.vector.tensor_tensor(
-                out=pre[c % 3][:, a0 * P:a1 * P].rearrange("q (a p t) -> q a p t", p=HW, t=T),
+                out=pre[c % 2][:, a0 * P:a1 * P].rearrange("q (a p t) -> q a p t", p=HW, t=T),
                 in0=u.unsqueeze(1).broadcast_to([P, n, HW, T]),
                 in1=vb[:, 32 * s + a0:32 * s + a1, :].unsqueeze(2).broadcast_to([P, n, HW, T]),
                 op=ADD,
@@ -235,17 +234,17 @@ def tile_reidrnself_pa_t_w8_kernel(tc, x_bytes, x_scale, g1_w_words, g1_w_scales
             s, half = G_HALVES[c]
             a0 = 32 * s + 16 * half
             nc.gpsimd.tensor_tensor(
-                out=pre[(c + 2) % 3][:, 0:16 * P].rearrange("q (a p t) -> q a p t", p=HW, t=T),
+                out=hg[c % 2][:].rearrange("q (a p t) -> q a p t", p=HW, t=T),
                 in0=usb[USB[s]][:].unsqueeze(1).broadcast_to([P, 16, HW, T]),
                 in1=vb[:, a0:a0 + 16, :].unsqueeze(2).broadcast_to([P, 16, HW, T]),
                 op=ADD,
             )
 
         def relu_v(c, a0, a1):
-            nc.vector.tensor_scalar_max(hv[c % 2][:, a0 * P:a1 * P], pre[c % 3][:, a0 * P:a1 * P], 0.0)
+            nc.vector.tensor_scalar_max(hv[c % 2][:, a0 * P:a1 * P], pre[c % 2][:, a0 * P:a1 * P], 0.0)
 
         def relu_g(c):
-            nc.scalar.activation(out=hg[c % 2][:], in_=pre[(c + 2) % 3][:, 0:16 * P], func=RELU)
+            nc.scalar.activation(out=hg[c % 2][:], in_=hg[c % 2][:], func=RELU)
 
         def chunk_h(k):
             i, r = k // 8, k % 8
@@ -271,33 +270,36 @@ def tile_reidrnself_pa_t_w8_kernel(tc, x_bytes, x_scale, g1_w_words, g1_w_scales
         def mm(u, tag=None):
             n = state["y"]
             state["y"] = n + 1
+            width = u["codes"].shape[-1]
             y = psum.tile([P, 512], F32, name="y%d" % n, tag=tag or "ybank%d" % (n % 2))
-            nc.tensor.matmul_mx(out=y[:], lhsT=w2[:].bitcast(FP8X4), lhsT_scale=w2s[:], rhs=u["codes"].bitcast(FP8X4), rhs_scale=u["scales"], start=True, stop=True)
+            nc.tensor.matmul_mx(out=y[:, 0:width], lhsT=w2[:].bitcast(FP8X4), lhsT_scale=w2s[:], rhs=u["codes"].bitcast(FP8X4), rhs_scale=u["scales"], start=True, stop=True)
             u["y"] = y
+            u["width"] = width
 
         def pass1(u, on_vector=False):
             ys = ring.tile([P, 512], F32, name="ys")
             u["ys"] = ys
+            n = u["width"]
             if on_vector:
-                nc.vector.tensor_scalar(out=ys[:], in0=u["y"][:], scalar1=b2f[:, 0:1], scalar2=0.0, op0=ADD, op1=MAX)
-                return
-            nc.scalar.activation(out=ys[:], in_=u["y"][:], func=RELU, bias=b2[:, 0:1])
+                nc.vector.tensor_scalar(out=ys[:, 0:n], in0=u["y"][:, 0:n], scalar1=b2f[:, 0:1], scalar2=0.0, op0=ADD, op1=MAX)
+            else:
+                nc.scalar.activation(out=ys[:, 0:n], in_=u["y"][:, 0:n], func=RELU, bias=b2[:, 0:1])
 
         def turn(u):
             tb = tmp_bank("tr")
-            for j in range(4):
+            for j in range(u["width"] // P):
                 nc.tensor.transpose(tb[:, j * P:(j + 1) * P], u["ys"][:, j * P:(j + 1) * P], ident[:])
             u["t"] = tb
 
         def pass2(u, on_vector=False):
-            o = ring.tile([P, 4, P], F32, name="o")
+            n = u["width"]
+            o = ring.tile([P, 512], F32, name="o")
             if on_vector:
-                nc.vector.tensor_copy(out=o[:], in_=u["t"][:].rearrange("q (j c) -> q j c", j=4))
+                nc.vector.tensor_copy(out=o[:, 0:n], in_=u["t"][:, 0:n])
             else:
-                nc.scalar.copy(out=o[:], in_=u["t"][:].rearrange("q (j c) -> q j c", j=4))
-            half = u["half"]
-            rows = out[u["s"]].rearrange("a p c -> (a p) c")[half * 512:(half + 1) * 512, :]
-            nc.sync.dma_start(out=rows.rearrange("(j q) c -> q j c", q=P), in_=o[:])
+                nc.scalar.copy(out=o[:, 0:n], in_=u["t"][:, 0:n])
+            rows = out[u["s"]].rearrange("a p c -> (a p) c")[u["pair"]:u["pair"] + n, :]
+            nc.sync.dma_start(out=rows.rearrange("(j q) c -> q j c", q=P), in_=o[:, 0:n].rearrange("q (j c) -> q j c", c=P))
 
         def epilogue(units, hq):
             n = len(units)
@@ -319,7 +321,6 @@ def tile_reidrnself_pa_t_w8_kernel(tc, x_bytes, x_scale, g1_w_words, g1_w_scales
             nc.scalar.dma_start(out=scale[:], in_=x_scale.rearrange("o (g q t) z -> q (o g) (t z)", q=P, t=T))
             nc.scalar.dma_start(out=b1[:], in_=g1_b.rearrange("(q t) -> q t", t=T))
             nc.scalar.dma_start(out=b2[:], in_=g2_b.rearrange("(q o) -> q o", o=1))
-            nc.scalar.dma_start(out=b1row[:], in_=g1_b.partition_broadcast(P))
             nc.vector.memset(warm[:], 0.0)
             nc.vector.memset(w1s[:].bitcast(I32), 0)
             nc.vector.memset(w2s[:].bitcast(I32), 0)
@@ -341,7 +342,6 @@ def tile_reidrnself_pa_t_w8_kernel(tc, x_bytes, x_scale, g1_w_words, g1_w_scales
                 nc.sync.dma_start(out=w2s[32 * q:32 * q + 4, :].bitcast(I32), in_=g2_w_scales[0, 4 * q:4 * q + 4, :].bitcast(I32))
 
             cast_on_vector(0)
-            nc.vector.tensor_copy(out=b2f[:], in_=b2[:])
             mul_x(0)
             quant_x(0)
             nc.vector.tensor_copy(out=w1sp[:].rearrange("q (t m) -> q t m", t=T), in_=w1s[:].rearrange("q (m t) -> q t m", t=T))
@@ -350,9 +350,10 @@ def tile_reidrnself_pa_t_w8_kernel(tc, x_bytes, x_scale, g1_w_words, g1_w_scales
                     out=w1p[g][:].bitcast(I32).rearrange("q (t m) -> q t m", t=T),
                     in_=w1[g][:].bitcast(I32).rearrange("q (m t) -> q t m", t=T),
                 )
+            nc.scalar.dma_start(out=b1row[64:128, :], in_=g1_b.partition_broadcast(64))
             cast_x(3)
             make_v(0)
-            bias_v(0)
+            bias_v(0, 0, 112)
             make_u(0)
             scale_on_scalar(3)
             cast_x(1)
@@ -374,59 +375,68 @@ def tile_reidrnself_pa_t_w8_kernel(tc, x_bytes, x_scale, g1_w_words, g1_w_scales
                 elif c == 1:
                     quant_x(1)
                 elif c == 2:
-                    mul_x(2)
                     quant_x(2)
                 if c >= 1:
                     k = c - 1
                     quant_v(k, 0, 1024)
                     for half in range(2):
-                        units.append({"codes": cv[k % 2][:, half * 512:(half + 1) * 512], "scales": sv[k % 2][:, half * 512:(half + 1) * 512], "s": V_SAMPLES[k], "half": half})
-                    quant_half(cg[k % 2], sg[k % 2], hg[k % 2])
-                    units.append({"codes": cg[k % 2][:], "scales": sg[k % 2][:], "s": G_HALVES[k][0], "half": G_HALVES[k][1]})
+                        units.append({"codes": cv[k % 2][:, half * 512:(half + 1) * 512], "scales": sv[k % 2][:, half * 512:(half + 1) * 512], "s": V_SAMPLES[k], "pair": half * 512})
                 for n in h_ready:
                     quant_half(ch[n % 2], sh[n % 2], hh[n % 2])
-                    units.append({"codes": ch[n % 2][:], "scales": sh[n % 2][:], "s": H_SAMPLES[n // 2], "half": n % 2})
+                    units.append({"codes": ch[n % 2][:], "scales": sh[n % 2][:], "s": H_SAMPLES[n // 2], "pair": n % 2 * 512})
+                if c >= 1:
+                    quant_half(cg[k % 2], sg[k % 2], hg[k % 2])
+                    units.append({"codes": cg[k % 2][:], "scales": sg[k % 2][:], "s": G_HALVES[k][0], "pair": G_HALVES[k][1] * 512})
+                else:
+                    bias_v(0, 112, P)
                 h_ready = []
                 relu_v(c, 0, 32)
-                if c < last - 1:
-                    relu_g(c)
+                relu_g(c)
                 if c == 0:
                     make_uv_h()
-                    bias_v(3)
+                    bias_v(3, 0, 64)
                     bias_v_h()
                     scale_on_scalar(1)
+                    scale_on_scalar(2)
                 elif c in (1, 2):
                     make_u(c)
                     make_v(c)
-                    bias_v(c)
+                    bias_v(c, 0, P)
                 done = sum(H_CHUNKS[:c])
                 hq = list(range(done, done + H_CHUNKS[c]))
                 h_ready = [k // 4 for k in hq if k % 4 == 3]
                 epilogue(units, hq)
 
             k = last - 1
+            nc.vector.tensor_copy(out=b2f[:], in_=b2[:])
             add_v(last, 0, 16)
-            quant_v(k, 0, 1024)
-            nc.vector.tensor_scalar_max(hg[k % 2][:], pre[(k + 2) % 3][:, 0:16 * P], 0.0)
-            relu_v(last, 0, 16)
             quant_half(cg[k % 2], sg[k % 2], hg[k % 2])
-            quant_v(last, 0, 512)
-            tail = [{"codes": cv[k % 2][:, half * 512:(half + 1) * 512], "scales": sv[k % 2][:, half * 512:(half + 1) * 512], "s": V_SAMPLES[k], "half": half} for half in range(2)]
-            tail.append({"codes": cg[k % 2][:], "scales": sg[k % 2][:], "s": G_HALVES[k][0], "half": G_HALVES[k][1]})
-            tail.append({"codes": cv[last % 2][:, 0:512], "scales": sv[last % 2][:, 0:512], "s": V_SAMPLES[last], "half": 0})
+            quant_v(k, 0, 1024)
+            relu_v(last, 0, 8)
+            relu_v(last, 8, 16)
+            quant_v(last, 0, 256)
+            quant_v(last, 256, 512)
+            tail = [{"codes": cg[k % 2][:], "scales": sg[k % 2][:], "s": G_HALVES[k][0], "pair": G_HALVES[k][1] * 512}]
+            tail += [{"codes": cv[k % 2][:, half * 512:(half + 1) * 512], "scales": sv[k % 2][:, half * 512:(half + 1) * 512], "s": V_SAMPLES[k], "pair": half * 512} for half in range(2)]
+            for half in range(2):
+                tail.append({"codes": cv[last % 2][:, half * 256:(half + 1) * 256], "scales": sv[last % 2][:, half * 256:(half + 1) * 256], "s": V_SAMPLES[last], "pair": half * 256})
             mm(tail[0], TAIL_TAGS[0])
-            mm(tail[1], TAIL_TAGS[1])
             pass1(tail[0])
-            pass1(tail[1])
             turn(tail[0])
+            mm(tail[1], TAIL_TAGS[1])
+            mm(tail[2], TAIL_TAGS[2])
+            pass1(tail[1])
             pass2(tail[0])
             turn(tail[1])
-            mm(tail[2], TAIL_TAGS[2])
-            pass2(tail[1])
             mm(tail[3], TAIL_TAGS[3])
-            pass1(tail[2])
-            pass1(tail[3], True)
+            mm(tail[4], TAIL_TAGS[4])
+            pass1(tail[2], True)
+            pass2(tail[1])
             turn(tail[2])
+            pass1(tail[3])
+            pass1(tail[4], True)
             turn(tail[3])
+            turn(tail[4])
             pass2(tail[2])
             pass2(tail[3], True)
+            pass2(tail[4])

@@ -12,7 +12,6 @@ FP8 = mybir.dt.float8_e4m3fn
 FP8X4 = mybir.dt.float8_e4m3fn_x4
 ADD = mybir.AluOpType.add
 MULT = mybir.AluOpType.mult
-MAX = mybir.AluOpType.max
 COPY = mybir.ActivationFunctionType.Copy
 RELU = mybir.ActivationFunctionType.Relu
 
@@ -21,14 +20,15 @@ P = 128
 T = 4
 FLOPS = 2 * MB * HW * C * K1 * 2 + 2 * MB * HW * HW * K1 * G2
 
+ON_V = [0, 1, 1, 0]
+RELU_G_ON_V = [0, 1, 0, 0, 1, 0, 0, 1, 0]
 H_CHUNKS = [2, 2, 2, 2, 2, 2, 2, 2, 0]
-X_ORDER = [0,"s","w",3,1,2]
+Y3 = 3
 
-V_SAMPLES = [0, 1, 2, 4, 5, 6, 8, 9, 10, 12]
-G_HALVES = [(3, 0), (3, 1), (7, 0), (7, 1), (11, 0), (11, 1), (13, 0), (13, 1), (12, 1)]
-H_SAMPLES = [14, 15]
+V_SAMPLES = [0, 1, 2, 4, 5, 6, 8, 9, 10, 14]
+G_HALVES = [(3, 0), (3, 1), (7, 0), (7, 1), (11, 0), (11, 1), (15, 0), (15, 1), (14, 1)]
+H_SAMPLES = [12, 13]
 TAIL_TAGS = ["ybank0", "ybank1", "ubank0", "ubank1", "ubank2"]
-USB = {3: 0, 7: 1, 11: 2, 12: 3, 13: 4}
 
 
 def tile_reidrnself_pa_t_w8_kernel(tc, x_bytes, x_scale, g1_w_words, g1_w_scales, g1_b, g2_w_words, g2_w_scales, g2_b, out):
@@ -44,22 +44,23 @@ def tile_reidrnself_pa_t_w8_kernel(tc, x_bytes, x_scale, g1_w_words, g1_w_scales
         xb = [keep.tile([P, 2 * 4 * P], U8, name="xb%d" % j) for j in range(4)]
         xw = [keep.tile([P, 2 * 4 * P], BF16, name="xw%d" % j) for j in range(4)]
         xg = [keep.tile([P, 2 * P * T], BF16, name="xg%d" % j, align_bytes=64) for j in range(4)]
-        xc = [keep.tile([P, 2 * P], U32, name="xc%d" % j, align_bytes=64) for j in range(4)]
-        xs = [keep.tile([P, 2 * P], U8, name="xs%d" % j, align_bytes=64) for j in range(4)]
-        xch = keep.tile([P, 2 * P], U32, name="xch", align_bytes=64)
-        xsh = keep.tile([P, 2 * P], U8, name="xsh", align_bytes=64)
+        xc03 = keep.tile([P, 4 * P], U32, name="xc03", align_bytes=64)
+        xs03 = keep.tile([P, 4 * P], U8, name="xs03", align_bytes=64)
+        xc12 = [keep.tile([P, 2 * P], U32, name="xc%d" % j, align_bytes=64) for j in (1, 2)]
+        xs12 = [keep.tile([P, 2 * P], U8, name="xs%d" % j, align_bytes=64) for j in (1, 2)]
         scale = keep.tile([P, 2, T], F32, name="scale")
         b1 = keep.tile([P, T], BF16, name="b1")
         b1row = keep.tile([P, K1], BF16, name="b1row")
         b2 = keep.tile([P, 1], BF16, name="b2")
+        b2row = keep.tile([P, G2], BF16, name="b2row")
         w1 = [keep.tile([P, K1], U32, name="w1raw%d" % g) for g in range(4)]
         w1p = [keep.tile([P, K1], U32, name="w1p%d" % g, align_bytes=64) for g in range(4)]
         w1s = keep.tile([P, K1], U8, name="w1s")
         w1sp = keep.tile([P, K1], U8, name="w1sp", align_bytes=64)
         w2 = keep.tile([P, G2], U32, name="w2", align_bytes=64)
         w2s = keep.tile([P, G2], U8, name="w2s", align_bytes=64)
-        vb = keep.tile([P, 448, T], F32, name="vb", align_bytes=64)
-        usb = [keep.tile([P, HW, T], F32, name="usb%d" % i, align_bytes=64) for i in range(5)]
+        vb = keep.tile([P, MB * HW, T], F32, name="vb", align_bytes=64)
+        usb = [keep.tile([P, 2 * HW, T], F32, name="usb%d" % i, align_bytes=64) for i in range(4)]
         uv = keep.tile([P, K1], F32, name="uv")
         sel = [keep.tile([P, HW * HW], F32, name="sel%d" % i) for i in range(2)]
         pre = [keep.tile([P, HW * HW * T], BF16, name="pre%d" % i, align_bytes=64) for i in range(2)]
@@ -72,17 +73,25 @@ def tile_reidrnself_pa_t_w8_kernel(tc, x_bytes, x_scale, g1_w_words, g1_w_scales
         sg = [keep.tile([P, HW * HW // 2], U8, name="sg%d" % i, align_bytes=64) for i in range(2)]
         ch = [keep.tile([P, HW * HW // 2], U32, name="ch%d" % i, align_bytes=64) for i in range(2)]
         sh = [keep.tile([P, HW * HW // 2], U8, name="sh%d" % i, align_bytes=64) for i in range(2)]
-        b2f = keep.tile([P, 1], F32, name="b2f")
         warm = keep.tile([P, 1], F32, name="warm")
         warm2 = keep.tile([P, 1], F32, name="warm2")
 
         ubank = {}
-        state = {"y": 0, "tmp": 0}
+        vbank = {}
+        state = {"n": 0}
 
-        def tmp_bank(name):
-            n = state["tmp"]
-            state["tmp"] = n + 1
-            return psum.tile([P, 512], F32, name="%s%d" % (name, n), tag="tmp", bufs=3)
+        def bank(tag, bufs=1):
+            state["n"] += 1
+            return psum.tile([P, 512], F32, name="%s_%d" % (tag, state["n"]), tag=tag, bufs=bufs)
+
+        def tmp_bank():
+            return bank("tmp", 3)
+
+        def x_codes(j, g, lo=0, n=P):
+            if j in (0, 3):
+                c0 = 2 * P * g + (P if j == 3 else 0) + lo
+                return xc03[:, c0:c0 + n], xs03[:, c0:c0 + n]
+            return xc12[j - 1][:, g * P:(g + 1) * P], xs12[j - 1][:, g * P:(g + 1) * P]
 
         def load_x(j):
             for g in range(2):
@@ -94,6 +103,9 @@ def tile_reidrnself_pa_t_w8_kernel(tc, x_bytes, x_scale, g1_w_words, g1_w_scales
         def cast_x(j):
             nc.scalar.copy(out=xw[j][:], in_=xb[j][:].bitcast(FP8))
 
+        def cast_on_vector(j):
+            nc.vector.tensor_copy(out=xw[j][:], in_=xb[j][:].bitcast(FP8))
+
         def scale_on_scalar(j):
             for g in range(2):
                 for t in range(T):
@@ -104,10 +116,7 @@ def tile_reidrnself_pa_t_w8_kernel(tc, x_bytes, x_scale, g1_w_words, g1_w_scales
                         scale=scale[:, g, t:t + 1],
                     )
 
-        def cast_on_vector(j):
-            nc.vector.tensor_copy(out=xw[j][:], in_=xb[j][:].bitcast(FP8))
-
-        def mul_x(j):
+        def scale_on_vector(j):
             for g in range(2):
                 nc.vector.tensor_tensor(
                     out=xg[j][:, g * 512:(g + 1) * 512].rearrange("q (b n t) -> q b n t", b=4, t=T),
@@ -116,64 +125,63 @@ def tile_reidrnself_pa_t_w8_kernel(tc, x_bytes, x_scale, g1_w_words, g1_w_scales
                     op=MULT,
                 )
 
+        def quant(codes, scales, values):
+            nc.vector.quantize_mx(out=codes.bitcast(FP8X4), scales=scales, in_=values)
+
         def quant_x(j):
-            nc.vector.quantize_mx(out=xc[j][:].bitcast(FP8X4), scales=xs[j][:], in_=xg[j][:])
+            if j in (0, 3):
+                for g in range(2):
+                    codes, scales = x_codes(j, g)
+                    quant(codes, scales, xg[j][:, g * 512:(g + 1) * 512])
+            else:
+                quant(xc12[j - 1][:], xs12[j - 1][:], xg[j][:])
 
-        def dup_h():
-            for k in range(2):
-                nc.vector.tensor_copy(
-                    out=xch[:].bitcast(I32).rearrange("q (g n) -> q g n", g=2)[:, :, 64 * k:64 * k + 64],
-                    in_=xc[3][:].bitcast(I32).rearrange("q (g n) -> q g n", g=2)[:, :, 64:128],
-                )
-                nc.vector.tensor_copy(
-                    out=xsh[:].rearrange("q (g n) -> q g n", g=2)[:, :, 64 * k:64 * k + 64],
-                    in_=xs[3][:].rearrange("q (g n) -> q g n", g=2)[:, :, 64:128],
-                )
-
-        def stage1(j, bank, first_group):
+        def stage1(j, ps, first_group):
             for t in range(T):
                 for g in range(2):
                     w = first_group + g
+                    codes, scales = x_codes(j, g)
                     nc.tensor.matmul_mx(
-                        out=bank[:, t * P:(t + 1) * P],
+                        out=ps[:, t * P:(t + 1) * P],
                         lhsT=w1p[w][:, t * P:(t + 1) * P].bitcast(FP8X4),
                         lhsT_scale=w1sp[4 * w:P, t * P:(t + 1) * P],
-                        rhs=xc[j][:, g * P:(g + 1) * P].bitcast(FP8X4),
-                        rhs_scale=xs[j][:, g * P:(g + 1) * P],
+                        rhs=codes.bitcast(FP8X4),
+                        rhs_scale=scales,
                         start=(g == 0),
                         stop=(g == 1),
                     )
 
-        def stage1_h(bank, first_group):
+        def stage1_h(ps, first_group, lo):
             for g in range(2):
                 w = first_group + g
+                codes, scales = x_codes(3, g, lo)
                 nc.tensor.matmul_mx(
-                    out=bank[:],
-                    lhsT=xch[:, g * P:(g + 1) * P].bitcast(FP8X4),
-                    lhsT_scale=xsh[:, g * P:(g + 1) * P],
+                    out=ps[:],
+                    lhsT=codes.bitcast(FP8X4),
+                    lhsT_scale=scales,
                     rhs=w1p[w][:].bitcast(FP8X4),
                     rhs_scale=w1sp[4 * w:P, :],
                     start=(g == 0),
                     stop=(g == 1),
                 )
 
-        def u_view(s):
-            return ubank[s // 4][:].rearrange("q (t r) -> q r t", t=T)[:, 32 * (s % 4):32 * (s % 4) + 32, :]
+        def u_rows(s, n=HW):
+            r = 32 * (s % 4)
+            return ubank[s // 4][:].rearrange("q (t r) -> q r t", t=T)[:, r:r + n, :]
+
+        def u_sbuf(s):
+            return usb[s // 4][:, 32 * (s % 2):32 * (s % 2) + 32, :] if s >= 12 else usb[s // 4][:, 0:HW, :]
 
         def make_u(j):
-            if j < 3:
-                ubank[j] = psum.tile([P, 512], F32, name="u_of_%d" % j, tag="ubank%d" % j)
-            else:
-                ubank[j] = tmp_bank("u_of_3_")
+            ubank[j] = bank("ubank%d" % j) if j < 3 else tmp_bank()
             stage1(j, ubank[j], 0)
-            for smp in USB:
-                if smp // 4 == j:
-                    nc.scalar.copy(out=usb[USB[smp]][:], in_=u_view(smp))
-
-        vbank = {}
+            if j < 3:
+                nc.scalar.copy(out=usb[j][:, 0:HW, :], in_=u_rows(4 * j + 3))
+            else:
+                nc.scalar.copy(out=usb[j][:], in_=u_rows(14, 2 * HW))
 
         def make_v(j):
-            vbank[j] = tmp_bank("v_of_%d_" % j)
+            vbank[j] = tmp_bank()
             stage1(j, vbank[j], 2)
 
         def bias_v(j, r0, r1):
@@ -185,11 +193,11 @@ def tile_reidrnself_pa_t_w8_kernel(tc, x_bytes, x_scale, g1_w_words, g1_w_scales
             )
 
         def make_uv_h():
-            bank = tmp_bank("uh")
-            stage1_h(bank, 0)
-            nc.scalar.copy(out=uv[0:64, :], in_=bank[0:64, :])
-            vbank["h"] = tmp_bank("vh")
-            stage1_h(vbank["h"], 2)
+            ub = tmp_bank()
+            stage1_h(ub, 0, 0)
+            nc.scalar.copy(out=uv[0:64, :], in_=ub[0:64, :])
+            vbank["h"] = tmp_bank()
+            stage1_h(vbank["h"], 2, -64)
 
         def bias_v_h():
             nc.vector.tensor_tensor(
@@ -222,7 +230,7 @@ def tile_reidrnself_pa_t_w8_kernel(tc, x_bytes, x_scale, g1_w_words, g1_w_scales
         def add_v(c, a0, a1):
             s = V_SAMPLES[c]
             n = a1 - a0
-            u = usb[USB[s]][:] if s in USB else u_view(s)
+            u = u_rows(s) if s < 12 else u_sbuf(s)
             nc.vector.tensor_tensor(
                 out=pre[c % 2][:, a0 * P:a1 * P].rearrange("q (a p t) -> q a p t", p=HW, t=T),
                 in0=u.unsqueeze(1).broadcast_to([P, n, HW, T]),
@@ -235,7 +243,7 @@ def tile_reidrnself_pa_t_w8_kernel(tc, x_bytes, x_scale, g1_w_words, g1_w_scales
             a0 = 32 * s + 16 * half
             nc.gpsimd.tensor_tensor(
                 out=hg[c % 2][:].rearrange("q (a p t) -> q a p t", p=HW, t=T),
-                in0=usb[USB[s]][:].unsqueeze(1).broadcast_to([P, 16, HW, T]),
+                in0=u_sbuf(s).unsqueeze(1).broadcast_to([P, 16, HW, T]),
                 in1=vb[:, a0:a0 + 16, :].unsqueeze(2).broadcast_to([P, 16, HW, T]),
                 op=ADD,
             )
@@ -244,77 +252,89 @@ def tile_reidrnself_pa_t_w8_kernel(tc, x_bytes, x_scale, g1_w_words, g1_w_scales
             nc.vector.tensor_scalar_max(hv[c % 2][:, a0 * P:a1 * P], pre[c % 2][:, a0 * P:a1 * P], 0.0)
 
         def relu_g(c):
-            nc.scalar.activation(out=hg[c % 2][:], in_=hg[c % 2][:], func=RELU)
+            if RELU_G_ON_V[c]:
+                nc.vector.tensor_scalar_max(hg[c % 2][:], hg[c % 2][:], 0.0)
+            else:
+                nc.scalar.activation(out=hg[c % 2][:], in_=hg[c % 2][:], func=RELU)
 
         def chunk_h(k):
             i, r = k // 8, k % 8
-            bank = tmp_bank("hc")
+            ps = tmp_bank()
             for t in range(T):
-                nc.tensor.matmul(bank[:, t * P:(t + 1) * P], lhsT=uv[:, t * P:(t + 1) * P], rhs=sel[i][:, r * P:(r + 1) * P], start=True, stop=True)
-            return bank
+                nc.tensor.matmul(ps[:, t * P:(t + 1) * P], lhsT=uv[:, t * P:(t + 1) * P], rhs=sel[i][:, r * P:(r + 1) * P], start=True, stop=True)
+            return ps
 
-        def relu_h(k, bank):
+        def relu_h(k, ps):
             r = k % 4
             nc.scalar.activation(
                 out=hh[(k // 4) % 2][:, r * 512:(r + 1) * 512].rearrange("q (n t) -> q n t", t=T),
-                in_=bank[:].rearrange("q (t n) -> q n t", t=T),
+                in_=ps[:].rearrange("q (t n) -> q n t", t=T),
                 func=RELU,
             )
 
-        def quant_v(c, p0, p1):
-            nc.vector.quantize_mx(out=cv[c % 2][:, p0:p1].bitcast(FP8X4), scales=sv[c % 2][:, p0:p1], in_=hv[c % 2][:, p0 * T:p1 * T])
+        def unit(codes, scales, s, pair, lo=0, n=512):
+            return {"codes": codes[:, lo:lo + n], "scales": scales[:, lo:lo + n], "s": s, "pair": pair, "n": n}
 
-        def quant_half(codes, scales, h):
-            nc.vector.quantize_mx(out=codes[:].bitcast(FP8X4), scales=scales[:], in_=h[:])
-
-        def mm(u, tag=None):
-            n = state["y"]
-            state["y"] = n + 1
-            width = u["codes"].shape[-1]
-            y = psum.tile([P, 512], F32, name="y%d" % n, tag=tag or "ybank%d" % (n % 2))
-            nc.tensor.matmul_mx(out=y[:, 0:width], lhsT=w2[:].bitcast(FP8X4), lhsT_scale=w2s[:], rhs=u["codes"].bitcast(FP8X4), rhs_scale=u["scales"], start=True, stop=True)
-            u["y"] = y
-            u["width"] = width
-
-        def pass1(u, on_vector=False):
-            ys = ring.tile([P, 512], F32, name="ys")
-            u["ys"] = ys
-            n = u["width"]
-            if on_vector:
-                nc.vector.tensor_scalar(out=ys[:, 0:n], in0=u["y"][:, 0:n], scalar1=b2f[:, 0:1], scalar2=0.0, op0=ADD, op1=MAX)
-            else:
-                nc.scalar.activation(out=ys[:, 0:n], in_=u["y"][:, 0:n], func=RELU, bias=b2[:, 0:1])
-
-        def turn(u):
-            tb = tmp_bank("tr")
-            for j in range(u["width"] // P):
-                nc.tensor.transpose(tb[:, j * P:(j + 1) * P], u["ys"][:, j * P:(j + 1) * P], ident[:])
-            u["t"] = tb
-
-        def pass2(u, on_vector=False):
-            n = u["width"]
-            o = ring.tile([P, 512], F32, name="o")
-            if on_vector:
-                nc.vector.tensor_copy(out=o[:, 0:n], in_=u["t"][:, 0:n])
-            else:
-                nc.scalar.copy(out=o[:, 0:n], in_=u["t"][:, 0:n])
+        def store(u, o):
+            n = u["n"]
             rows = out[u["s"]].rearrange("a p c -> (a p) c")[u["pair"]:u["pair"] + n, :]
             nc.sync.dma_start(out=rows.rearrange("(j q) c -> q j c", q=P), in_=o[:, 0:n].rearrange("q (j c) -> q j c", c=P))
 
-        def epilogue(units, hq):
+        def mm(u, tag):
+            u["y"] = bank(tag)
+            nc.tensor.matmul_mx(out=u["y"][:], lhsT=w2[:].bitcast(FP8X4), lhsT_scale=w2s[:], rhs=u["codes"].bitcast(FP8X4), rhs_scale=u["scales"], start=True, stop=True)
+
+        def pass1(u):
+            u["ys"] = ring.tile([P, 512], F32, name="ys")
+            nc.scalar.activation(out=u["ys"][:], in_=u["y"][:], func=RELU, bias=b2[:, 0:1])
+
+        def turn(u):
+            u["t"] = tmp_bank()
+            for j in range(4):
+                nc.tensor.transpose(u["t"][:, j * P:(j + 1) * P], u["ys"][:, j * P:(j + 1) * P], ident[:])
+
+        def pass2(u):
+            o = ring.tile([P, 512], F32, name="o")
+            nc.scalar.copy(out=o[:], in_=u["t"][:])
+            store(u, o)
+
+        def mm_rows(u, tag):
+            u["y"] = bank(tag)
+            for j in range(u["n"] // P):
+                cols = slice(j * P, (j + 1) * P)
+                nc.tensor.matmul_mx(out=u["y"][:, cols], lhsT=u["codes"][:, cols].bitcast(FP8X4), lhsT_scale=u["scales"][:, cols], rhs=w2[:].bitcast(FP8X4), rhs_scale=w2s[:], start=True, stop=True)
+
+        def finish_rows(u):
+            n = u["n"]
+            ys = ring.tile([P, 512], F32, name="yr")
+            o = ring.tile([P, 512], F32, name="o2")
+            nc.vector.tensor_tensor(
+                out=ys[:, 0:n].rearrange("q (j c) -> q j c", c=P),
+                in0=u["y"][:, 0:n].rearrange("q (j c) -> q j c", c=P),
+                in1=b2row[:].unsqueeze(1).broadcast_to([P, n // P, P]),
+                op=ADD,
+            )
+            nc.vector.tensor_scalar_max(o[:, 0:n], ys[:, 0:n], 0.0)
+            store(u, o)
+
+        def epilogue(units, hq, c):
             n = len(units)
-            for k, bank in [(k, chunk_h(k)) for k in hq]:
-                relu_h(k, bank)
-            for u in units[:2]:
-                mm(u)
+            for k, ps in [(k, chunk_h(k)) for k in hq]:
+                relu_h(k, ps)
+            ytags = ["ybank0", "ybank1", "ubank0"] if c >= Y3 else ["ybank0", "ybank1"]
+            d = len(ytags)
+            for i, u in enumerate(units[:d]):
+                mm(u, ytags[i])
             for u in units[:2]:
                 pass1(u)
             for i in range(n):
                 turn(units[i])
-                if i + 2 < n:
-                    mm(units[i + 2])
+                if i + d < n:
+                    mm(units[i + d], ytags[i])
+                if i + 2 < n and d > 2:
+                    pass1(units[i + 2])
                 pass2(units[i])
-                if i + 2 < n:
+                if i + 2 < n and d == 2:
                     pass1(units[i + 2])
 
         with tc.manual_schedule():
@@ -324,25 +344,24 @@ def tile_reidrnself_pa_t_w8_kernel(tc, x_bytes, x_scale, g1_w_words, g1_w_scales
             nc.vector.memset(warm[:], 0.0)
             nc.vector.memset(w1s[:].bitcast(I32), 0)
             nc.vector.memset(w2s[:].bitcast(I32), 0)
-            nc.scalar.activation(out=warm2[:], in_=warm[:], func=RELU)
             nc.vector.memset(sel[1][:], 0.0)
+            nc.scalar.activation(out=warm2[:], in_=warm[:], func=RELU)
             make_sel_g(0)
             make_sel_s(1)
-            for item in X_ORDER:
-                if item == "s":
-                    for q in range(4):
-                        nc.sync.dma_start(out=w1s[32 * q:32 * q + 16, :].bitcast(I32), in_=g1_w_scales[:, 4 * q:4 * q + 4, :].bitcast(I32))
-                elif item == "w":
-                    for g in (2, 3, 0, 1):
-                        nc.sync.dma_start(out=w1[g][:].bitcast(I32), in_=g1_w_words[g].rearrange("q n t -> q (n t)").bitcast(I32))
-                else:
-                    load_x(item)
+            load_x(0)
+            for q in range(4):
+                nc.sync.dma_start(out=w1s[32 * q:32 * q + 16, :].bitcast(I32), in_=g1_w_scales[:, 4 * q:4 * q + 4, :].bitcast(I32))
+            for g in (2, 3, 0, 1):
+                nc.sync.dma_start(out=w1[g][:].bitcast(I32), in_=g1_w_words[g].rearrange("q n t -> q (n t)").bitcast(I32))
+            load_x(3)
+            load_x(1)
+            load_x(2)
             nc.sync.dma_start(out=w2[:].bitcast(I32), in_=g2_w_words[0].rearrange("q n t -> q (n t)").bitcast(I32))
             for q in range(4):
                 nc.sync.dma_start(out=w2s[32 * q:32 * q + 4, :].bitcast(I32), in_=g2_w_scales[0, 4 * q:4 * q + 4, :].bitcast(I32))
 
             cast_on_vector(0)
-            mul_x(0)
+            scale_on_vector(0)
             quant_x(0)
             nc.vector.tensor_copy(out=w1sp[:].rearrange("q (t m) -> q t m", t=T), in_=w1s[:].rearrange("q (m t) -> q t m", t=T))
             for g in (2, 3, 0, 1):
@@ -355,88 +374,84 @@ def tile_reidrnself_pa_t_w8_kernel(tc, x_bytes, x_scale, g1_w_words, g1_w_scales
             make_v(0)
             bias_v(0, 0, 112)
             make_u(0)
-            scale_on_scalar(3)
+            if not ON_V[3]:
+                scale_on_scalar(3)
             cast_x(1)
             cast_x(2)
+            nc.scalar.dma_start(out=b2row[:], in_=g2_b.partition_broadcast(P))
 
             last = len(V_SAMPLES) - 1
-            n_g = len(G_HALVES)
             h_ready = []
             for c in range(last):
+                k = c - 1
                 units = []
                 add_v(c, 0, 32)
-                if c < n_g:
-                    add_g(c)
+                add_g(c)
+                if c == 1:
+                    bias_v(3, 64, 128)
+                for j in (1, 2):
+                    if c == j:
+                        if ON_V[j]:
+                            scale_on_vector(j)
+                        quant_x(j)
                 if c == 0:
+                    if ON_V[3]:
+                        scale_on_vector(3)
                     quant_x(3)
-                    dup_h()
+                    bias_v(0, 112, P)
+                    make_uv_h()
                     make_u(3)
                     make_v(3)
-                elif c == 1:
-                    quant_x(1)
-                elif c == 2:
-                    quant_x(2)
-                if c >= 1:
-                    k = c - 1
-                    quant_v(k, 0, 1024)
-                    for half in range(2):
-                        units.append({"codes": cv[k % 2][:, half * 512:(half + 1) * 512], "scales": sv[k % 2][:, half * 512:(half + 1) * 512], "s": V_SAMPLES[k], "pair": half * 512})
-                for n in h_ready:
-                    quant_half(ch[n % 2], sh[n % 2], hh[n % 2])
-                    units.append({"codes": ch[n % 2][:], "scales": sh[n % 2][:], "s": H_SAMPLES[n // 2], "pair": n % 2 * 512})
-                if c >= 1:
-                    quant_half(cg[k % 2], sg[k % 2], hg[k % 2])
-                    units.append({"codes": cg[k % 2][:], "scales": sg[k % 2][:], "s": G_HALVES[k][0], "pair": G_HALVES[k][1] * 512})
                 else:
-                    bias_v(0, 112, P)
-                h_ready = []
+                    if RELU_G_ON_V[k]:
+                        relu_g(k)
+                    quant(cv[k % 2][:], sv[k % 2][:], hv[k % 2][:])
+                    units += [unit(cv[k % 2], sv[k % 2], V_SAMPLES[k], 512 * half, 512 * half) for half in range(2)]
+                for n in h_ready:
+                    quant(ch[n % 2][:], sh[n % 2][:], hh[n % 2][:])
+                    units.append(unit(ch[n % 2], sh[n % 2], H_SAMPLES[n // 2], n % 2 * 512))
+                if c >= 1:
+                    quant(cg[k % 2][:], sg[k % 2][:], hg[k % 2][:])
+                    units.append(unit(cg[k % 2], sg[k % 2], G_HALVES[k][0], 512 * G_HALVES[k][1]))
                 relu_v(c, 0, 32)
-                relu_g(c)
+                if not RELU_G_ON_V[c]:
+                    relu_g(c)
                 if c == 0:
-                    make_uv_h()
-                    bias_v(3, 0, 64)
                     bias_v_h()
-                    scale_on_scalar(1)
-                    scale_on_scalar(2)
+                    for j in (1, 2):
+                        if not ON_V[j]:
+                            scale_on_scalar(j)
                 elif c in (1, 2):
                     make_u(c)
                     make_v(c)
                     bias_v(c, 0, P)
                 done = sum(H_CHUNKS[:c])
                 hq = list(range(done, done + H_CHUNKS[c]))
-                h_ready = [k // 4 for k in hq if k % 4 == 3]
-                epilogue(units, hq)
+                h_ready = [n // 4 for n in hq if n % 4 == 3]
+                epilogue(units, hq, c)
 
             k = last - 1
-            nc.vector.tensor_copy(out=b2f[:], in_=b2[:])
             add_v(last, 0, 16)
-            quant_half(cg[k % 2], sg[k % 2], hg[k % 2])
-            quant_v(k, 0, 1024)
+            quant(cg[k % 2][:], sg[k % 2][:], hg[k % 2][:])
+            quant(cv[k % 2][:], sv[k % 2][:], hv[k % 2][:])
             relu_v(last, 0, 8)
             relu_v(last, 8, 16)
-            quant_v(last, 0, 256)
-            quant_v(last, 256, 512)
-            tail = [{"codes": cg[k % 2][:], "scales": sg[k % 2][:], "s": G_HALVES[k][0], "pair": G_HALVES[k][1] * 512}]
-            tail += [{"codes": cv[k % 2][:, half * 512:(half + 1) * 512], "scales": sv[k % 2][:, half * 512:(half + 1) * 512], "s": V_SAMPLES[k], "pair": half * 512} for half in range(2)]
             for half in range(2):
-                tail.append({"codes": cv[last % 2][:, half * 256:(half + 1) * 256], "scales": sv[last % 2][:, half * 256:(half + 1) * 256], "s": V_SAMPLES[last], "pair": half * 256})
+                quant(cv[last % 2][:, half * 256:(half + 1) * 256], sv[last % 2][:, half * 256:(half + 1) * 256], hv[last % 2][:, half * 1024:(half + 1) * 1024])
+            tail = [unit(cg[k % 2], sg[k % 2], G_HALVES[k][0], 512 * G_HALVES[k][1])]
+            tail += [unit(cv[k % 2], sv[k % 2], V_SAMPLES[k], 512 * half, 512 * half) for half in range(2)]
+            tail += [unit(cv[last % 2], sv[last % 2], V_SAMPLES[last], 256 * half, 256 * half, 256) for half in range(2)]
             mm(tail[0], TAIL_TAGS[0])
+            mm(tail[1], TAIL_TAGS[1])
+            mm_rows(tail[2], TAIL_TAGS[2])
             pass1(tail[0])
             turn(tail[0])
-            mm(tail[1], TAIL_TAGS[1])
-            mm(tail[2], TAIL_TAGS[2])
             pass1(tail[1])
             pass2(tail[0])
+            mm_rows(tail[3], TAIL_TAGS[3])
+            mm_rows(tail[4], TAIL_TAGS[4])
             turn(tail[1])
-            mm(tail[3], TAIL_TAGS[3])
-            mm(tail[4], TAIL_TAGS[4])
-            pass1(tail[2], True)
             pass2(tail[1])
-            turn(tail[2])
-            pass1(tail[3])
-            pass1(tail[4], True)
-            turn(tail[3])
-            turn(tail[4])
-            pass2(tail[2])
-            pass2(tail[3], True)
-            pass2(tail[4])
+            finish_rows(tail[2])
+            finish_rows(tail[3])
+            finish_rows(tail[4])

@@ -18,17 +18,24 @@ RELU = mybir.ActivationFunctionType.Relu
 MB, C, HW, K1, G2 = 16, 1024, 32, 512, 128
 P = 128
 T = 4
-FLOPS = 2 * MB * HW * C * K1 * 2 + 2 * MB * HW * HW * K1 * G2
+GROUP = 4
+PAIRS = HW * HW
+UNIT = 512
+A_UNIT = UNIT // HW
+BANK = 512
+CHUNK = 128
 
-ON_V = [0, 1, 1, 0]
-RELU_G_ON_V = [0, 1, 0, 0, 1, 0, 0, 1, 0]
-H_CHUNKS = [2, 2, 2, 2, 2, 2, 2, 2, 0]
-Y3 = 3
+FLOPS = 2 * MB * HW * C * K1 * 2 + 2 * MB * PAIRS * K1 * G2
 
-V_SAMPLES = [0, 1, 2, 4, 5, 6, 8, 9, 10, 14]
-G_HALVES = [(3, 0), (3, 1), (7, 0), (7, 1), (11, 0), (11, 1), (15, 0), (15, 1), (14, 1)]
-H_SAMPLES = [12, 13]
-TAIL_TAGS = ["ybank0", "ybank1", "ubank0", "ubank1", "ubank2"]
+VECTOR_SAMPLES = [0, 1, 2, 4, 5, 6, 8, 9, 10, 14]
+GPSIMD_HALVES = [(3, 0), (3, 1), (7, 0), (7, 1), (11, 0), (11, 1), (15, 0), (15, 1), (14, 1)]
+TENSOR_SAMPLES = [12, 13]
+STEPS = len(GPSIMD_HALVES)
+CHUNKS_A_STEP = 2
+CHUNKS_A_UNIT = UNIT // CHUNK
+SAMPLE_CHUNKS = PAIRS // CHUNK
+LAST_SCALAR_RELU = STEPS - 3
+FREE_BANK_STEP = 3
 
 
 def tile_reidrnself_pa_t_w8_kernel(tc, x_bytes, x_scale, g1_w_words, g1_w_scales, g1_b, g2_w_words, g2_w_scales, g2_b, out):
@@ -41,417 +48,462 @@ def tile_reidrnself_pa_t_w8_kernel(tc, x_bytes, x_scale, g1_w_words, g1_w_scales
         ident = keep.tile([P, P], F32, name="ident")
         make_identity(nc, ident[:])
 
-        xb = [keep.tile([P, 2 * 4 * P], U8, name="xb%d" % j) for j in range(4)]
-        xw = [keep.tile([P, 2 * 4 * P], BF16, name="xw%d" % j) for j in range(4)]
+        xb = [keep.tile([P, 2 * GROUP * P], U8, name="xb%d" % j) for j in range(4)]
+        xw = [keep.tile([P, 2 * GROUP * P], BF16, name="xw%d" % j) for j in range(4)]
         xg = [keep.tile([P, 2 * P * T], BF16, name="xg%d" % j, align_bytes=64) for j in range(4)]
         xc03 = keep.tile([P, 4 * P], U32, name="xc03", align_bytes=64)
         xs03 = keep.tile([P, 4 * P], U8, name="xs03", align_bytes=64)
         xc12 = [keep.tile([P, 2 * P], U32, name="xc%d" % j, align_bytes=64) for j in (1, 2)]
         xs12 = [keep.tile([P, 2 * P], U8, name="xs%d" % j, align_bytes=64) for j in (1, 2)]
-        scale = keep.tile([P, 2, T], F32, name="scale")
-        b1 = keep.tile([P, T], BF16, name="b1")
-        b1row = keep.tile([P, K1], BF16, name="b1row")
-        b2 = keep.tile([P, 1], BF16, name="b2")
-        b2row = keep.tile([P, G2], BF16, name="b2row")
-        w1 = [keep.tile([P, K1], U32, name="w1raw%d" % g) for g in range(4)]
-        w1p = [keep.tile([P, K1], U32, name="w1p%d" % g, align_bytes=64) for g in range(4)]
+        x_scales = keep.tile([P, 2, T], F32, name="x_scales")
+
+        w1 = [keep.tile([P, 2 * K1], U32, name="w1raw%d" % i) for i in range(2)]
+        w1p = [keep.tile([P, 2 * K1], U32, name="w1p%d" % i, align_bytes=64) for i in range(2)]
         w1s = keep.tile([P, K1], U8, name="w1s")
         w1sp = keep.tile([P, K1], U8, name="w1sp", align_bytes=64)
         w2 = keep.tile([P, G2], U32, name="w2", align_bytes=64)
         w2s = keep.tile([P, G2], U8, name="w2s", align_bytes=64)
-        vb = keep.tile([P, MB * HW, T], F32, name="vb", align_bytes=64)
-        usb = [keep.tile([P, 2 * HW, T], F32, name="usb%d" % i, align_bytes=64) for i in range(4)]
-        uv = keep.tile([P, K1], F32, name="uv")
-        sel = [keep.tile([P, HW * HW], F32, name="sel%d" % i) for i in range(2)]
-        pre = [keep.tile([P, HW * HW * T], BF16, name="pre%d" % i, align_bytes=64) for i in range(2)]
-        hv = [keep.tile([P, HW * HW * T], BF16, name="hv%d" % i, align_bytes=64) for i in range(2)]
-        hg = [keep.tile([P, HW * HW * T // 2], BF16, name="hg%d" % i, align_bytes=64) for i in range(2)]
-        hh = [keep.tile([P, HW * HW * T // 2], BF16, name="hh%d" % i, align_bytes=64) for i in range(2)]
-        cv = [keep.tile([P, HW * HW], U32, name="cv%d" % i, align_bytes=64) for i in range(2)]
-        sv = [keep.tile([P, HW * HW], U8, name="sv%d" % i, align_bytes=64) for i in range(2)]
-        cg = [keep.tile([P, HW * HW // 2], U32, name="cg%d" % i, align_bytes=64) for i in range(2)]
-        sg = [keep.tile([P, HW * HW // 2], U8, name="sg%d" % i, align_bytes=64) for i in range(2)]
-        ch = [keep.tile([P, HW * HW // 2], U32, name="ch%d" % i, align_bytes=64) for i in range(2)]
-        sh = [keep.tile([P, HW * HW // 2], U8, name="sh%d" % i, align_bytes=64) for i in range(2)]
-        warm = keep.tile([P, 1], F32, name="warm")
-        warm2 = keep.tile([P, 1], F32, name="warm2")
+        b1 = keep.tile([P, T], BF16, name="b1")
+        b1row = keep.tile([P, K1], BF16, name="b1row")
+        b2 = keep.tile([P, 1], BF16, name="b2")
+        b2row = keep.tile([P, G2], BF16, name="b2row")
 
-        ubank = {}
-        vbank = {}
-        state = {"n": 0}
+        vb = keep.tile([P, MB * HW, T], F32, name="vb", align_bytes=64)
+        usb = [keep.tile([P, 2 * HW, T], F32, name="usb%d" % j, align_bytes=64) for j in range(4)]
+        uv = keep.tile([P, K1], F32, name="uv")
+        select = [keep.tile([P, PAIRS], F32, name="select%d" % i) for i in range(2)]
+
+        pre = [keep.tile([P, PAIRS * T], BF16, name="pre%d" % i, align_bytes=64) for i in range(2)]
+        hv = [keep.tile([P, PAIRS * T], BF16, name="hv%d" % i, align_bytes=64) for i in range(2)]
+        hg = [keep.tile([P, UNIT * T], BF16, name="hg%d" % i, align_bytes=64) for i in range(2)]
+        ht = [keep.tile([P, UNIT * T], BF16, name="ht%d" % i, align_bytes=64) for i in range(2)]
+        cv = [keep.tile([P, PAIRS], U32, name="cv%d" % i, align_bytes=64) for i in range(2)]
+        sv = [keep.tile([P, PAIRS], U8, name="sv%d" % i, align_bytes=64) for i in range(2)]
+        cg = [keep.tile([P, UNIT], U32, name="cg%d" % i, align_bytes=64) for i in range(2)]
+        sg = [keep.tile([P, UNIT], U8, name="sg%d" % i, align_bytes=64) for i in range(2)]
+        ct = [keep.tile([P, UNIT], U32, name="ct%d" % i, align_bytes=64) for i in range(2)]
+        st = [keep.tile([P, UNIT], U8, name="st%d" % i, align_bytes=64) for i in range(2)]
+        warm_in = keep.tile([P, 1], F32, name="warm_in")
+        warm_out = keep.tile([P, 1], F32, name="warm_out")
+
+        banks_made = []
 
         def bank(tag, bufs=1):
-            state["n"] += 1
-            return psum.tile([P, 512], F32, name="%s_%d" % (tag, state["n"]), tag=tag, bufs=bufs)
+            banks_made.append(tag)
+            return psum.tile([P, BANK], F32, name="%s_%d" % (tag, len(banks_made)), tag=tag, bufs=bufs)
 
-        def tmp_bank():
-            return bank("tmp", 3)
+        def rotating_bank():
+            return bank("rotating", 3)
 
-        def x_codes(j, g, lo=0, n=P):
-            if j in (0, 3):
-                c0 = 2 * P * g + (P if j == 3 else 0) + lo
-                return xc03[:, c0:c0 + n], xs03[:, c0:c0 + n]
-            return xc12[j - 1][:, g * P:(g + 1) * P], xs12[j - 1][:, g * P:(g + 1) * P]
+        u_bank = {}
+        v_bank = {}
+
 
         def load_x(j):
-            for g in range(2):
-                nc.sync.dma_start(
-                    out=xb[j][:, g * 512:(g + 1) * 512].rearrange("q (b n) -> q b n", b=4),
-                    in_=x_bytes[4 * j:4 * j + 4, g * 512:(g + 1) * 512, :].rearrange("b (q t) n -> q b (t n)", t=T),
-                )
+            nc.sync.dma_start(
+                out=xb[j][:].rearrange("q (b n) -> q b n", b=2 * GROUP),
+                in_=x_bytes[GROUP * j:GROUP * (j + 1)].rearrange("b (g q t) n -> q (b g) (t n)", g=2, t=T),
+            )
 
-        def cast_x(j):
+        def widen_on_scalar(j):
             nc.scalar.copy(out=xw[j][:], in_=xb[j][:].bitcast(FP8))
 
-        def cast_on_vector(j):
+        def widen_on_vector(j):
             nc.vector.tensor_copy(out=xw[j][:], in_=xb[j][:].bitcast(FP8))
+
+        def widened(j, g):
+            return xw[j][:].rearrange("q (b g t n) -> q g b n t", b=GROUP, g=2, t=T)[:, g]
+
+        def scaled(j, g):
+            return xg[j][:, g * P * T:(g + 1) * P * T].rearrange("q (b n t) -> q b n t", b=GROUP, t=T)
 
         def scale_on_scalar(j):
             for g in range(2):
                 for t in range(T):
                     nc.scalar.activation(
-                        out=xg[j][:, g * 512:(g + 1) * 512].rearrange("q (b n t) -> q t b n", b=4, t=T)[:, t, :, :],
-                        in_=xw[j][:, g * 512:(g + 1) * 512].rearrange("q (b t n) -> q t b n", b=4, t=T)[:, t, :, :],
+                        out=scaled(j, g)[:, :, :, t],
+                        in_=widened(j, g)[:, :, :, t],
                         func=COPY,
-                        scale=scale[:, g, t:t + 1],
+                        scale=x_scales[:, g, t:t + 1],
                     )
 
         def scale_on_vector(j):
             for g in range(2):
                 nc.vector.tensor_tensor(
-                    out=xg[j][:, g * 512:(g + 1) * 512].rearrange("q (b n t) -> q b n t", b=4, t=T),
-                    in0=xw[j][:, g * 512:(g + 1) * 512].rearrange("q (b t n) -> q b n t", b=4, t=T),
-                    in1=scale[:, g, :].unsqueeze(1).unsqueeze(1).broadcast_to([P, 4, HW, T]),
+                    out=scaled(j, g),
+                    in0=widened(j, g),
+                    in1=x_scales[:, g, :].unsqueeze(1).unsqueeze(1).broadcast_to([P, GROUP, HW, T]),
                     op=MULT,
                 )
 
-        def quant(codes, scales, values):
+        def quantize(codes, scales, values):
             nc.vector.quantize_mx(out=codes.bitcast(FP8X4), scales=scales, in_=values)
 
-        def quant_x(j):
+        def x_operand(j, g, shift=0):
+            if j in (0, 3):
+                lo = 2 * P * g + (P if j == 3 else 0) + shift
+                return xc03[:, lo:lo + P], xs03[:, lo:lo + P]
+            return xc12[j - 1][:, g * P:(g + 1) * P], xs12[j - 1][:, g * P:(g + 1) * P]
+
+        def quantize_x(j):
             if j in (0, 3):
                 for g in range(2):
-                    codes, scales = x_codes(j, g)
-                    quant(codes, scales, xg[j][:, g * 512:(g + 1) * 512])
+                    codes, scales = x_operand(j, g)
+                    quantize(codes, scales, xg[j][:, g * P * T:(g + 1) * P * T])
             else:
-                quant(xc12[j - 1][:], xs12[j - 1][:], xg[j][:])
+                quantize(xc12[j - 1][:], xs12[j - 1][:], xg[j][:])
 
-        def stage1(j, ps, first_group):
+
+        def w1_operand(w, lo, n):
+            return w1p[w // 2][:, w % 2 * K1 + lo:w % 2 * K1 + lo + n], w1sp[4 * w:P, lo:lo + n]
+
+        def channels_on_partitions(j, ps, first_w):
             for t in range(T):
                 for g in range(2):
-                    w = first_group + g
-                    codes, scales = x_codes(j, g)
+                    w_codes, w_scales = w1_operand(first_w + g, t * P, P)
+                    codes, scales = x_operand(j, g)
                     nc.tensor.matmul_mx(
                         out=ps[:, t * P:(t + 1) * P],
-                        lhsT=w1p[w][:, t * P:(t + 1) * P].bitcast(FP8X4),
-                        lhsT_scale=w1sp[4 * w:P, t * P:(t + 1) * P],
+                        lhsT=w_codes.bitcast(FP8X4),
+                        lhsT_scale=w_scales,
                         rhs=codes.bitcast(FP8X4),
                         rhs_scale=scales,
                         start=(g == 0),
                         stop=(g == 1),
                     )
 
-        def stage1_h(ps, first_group, lo):
+        def rows_on_partitions(ps, first_w, shift):
             for g in range(2):
-                w = first_group + g
-                codes, scales = x_codes(3, g, lo)
+                w_codes, w_scales = w1_operand(first_w + g, 0, K1)
+                codes, scales = x_operand(3, g, shift)
                 nc.tensor.matmul_mx(
                     out=ps[:],
                     lhsT=codes.bitcast(FP8X4),
                     lhsT_scale=scales,
-                    rhs=w1p[w][:].bitcast(FP8X4),
-                    rhs_scale=w1sp[4 * w:P, :],
+                    rhs=w_codes.bitcast(FP8X4),
+                    rhs_scale=w_scales,
                     start=(g == 0),
                     stop=(g == 1),
                 )
 
-        def u_rows(s, n=HW):
-            r = 32 * (s % 4)
-            return ubank[s // 4][:].rearrange("q (t r) -> q r t", t=T)[:, r:r + n, :]
+        def u_in_psum(s, n=HW):
+            r = HW * (s % GROUP)
+            return u_bank[s // GROUP][:].rearrange("q (t r) -> q r t", t=T)[:, r:r + n, :]
 
-        def u_sbuf(s):
-            return usb[s // 4][:, 32 * (s % 2):32 * (s % 2) + 32, :] if s >= 12 else usb[s // 4][:, 0:HW, :]
+        def u_in_sbuf(s):
+            r = HW * (s % 2) if s >= 3 * GROUP else 0
+            return usb[s // GROUP][:, r:r + HW, :]
 
         def make_u(j):
-            ubank[j] = bank("ubank%d" % j) if j < 3 else tmp_bank()
-            stage1(j, ubank[j], 0)
+            u_bank[j] = bank("u_of_group_%d" % j) if j < 3 else rotating_bank()
+            channels_on_partitions(j, u_bank[j], 0)
             if j < 3:
-                nc.scalar.copy(out=usb[j][:, 0:HW, :], in_=u_rows(4 * j + 3))
+                nc.scalar.copy(out=usb[j][:, 0:HW, :], in_=u_in_psum(GROUP * j + 3))
             else:
-                nc.scalar.copy(out=usb[j][:], in_=u_rows(14, 2 * HW))
+                nc.scalar.copy(out=usb[j][:], in_=u_in_psum(14, 2 * HW))
 
         def make_v(j):
-            vbank[j] = tmp_bank()
-            stage1(j, vbank[j], 2)
+            v_bank[j] = rotating_bank()
+            channels_on_partitions(j, v_bank[j], 2)
 
-        def bias_v(j, r0, r1):
+        def add_bias_1(j, r0, r1):
             nc.vector.tensor_tensor(
                 out=vb[:, j * P + r0:j * P + r1, :],
-                in0=vbank[j][:].rearrange("q (t r) -> q r t", t=T)[:, r0:r1, :],
+                in0=v_bank[j][:].rearrange("q (t r) -> q r t", t=T)[:, r0:r1, :],
                 in1=b1[:].unsqueeze(1).broadcast_to([P, r1 - r0, T]),
                 op=ADD,
             )
 
-        def make_uv_h():
-            ub = tmp_bank()
-            stage1_h(ub, 0, 0)
-            nc.scalar.copy(out=uv[0:64, :], in_=ub[0:64, :])
-            vbank["h"] = tmp_bank()
-            stage1_h(vbank["h"], 2, -64)
+        def make_uv():
+            ps = rotating_bank()
+            rows_on_partitions(ps, 0, 0)
+            nc.scalar.copy(out=uv[0:64, :], in_=ps[0:64, :])
+            v_bank["rows"] = rotating_bank()
+            rows_on_partitions(v_bank["rows"], 2, -64)
 
-        def bias_v_h():
+        def add_bias_1_rows():
             nc.vector.tensor_tensor(
                 out=uv[64:128, :].rearrange("q (t m) -> q t m", t=T),
-                in0=vbank["h"][64:128, :].rearrange("q (t m) -> q t m", t=T),
+                in0=v_bank["rows"][64:128, :].rearrange("q (t m) -> q t m", t=T),
                 in1=b1row[64:128, :].rearrange("q (m t) -> q t m", t=T),
                 op=ADD,
             )
 
-        def make_sel_g(i):
+
+        def make_select_on_gpsimd(i):
             nc.gpsimd.tensor_tensor(
-                out=sel[i][:].rearrange("q (a p) -> q a p", p=HW),
-                in0=ident[:, 32 * i:32 * i + 32].unsqueeze(1).broadcast_to([P, HW, HW]),
-                in1=ident[:, 64 + 32 * i:64 + 32 * i + 32].unsqueeze(2).broadcast_to([P, HW, HW]),
+                out=select[i][:].rearrange("q (a p) -> q a p", p=HW),
+                in0=ident[:, HW * i:HW * (i + 1)].unsqueeze(1).broadcast_to([P, HW, HW]),
+                in1=ident[:, 64 + HW * i:64 + HW * (i + 1)].unsqueeze(2).broadcast_to([P, HW, HW]),
                 op=ADD,
             )
 
-        def make_sel_s(i):
-            r0 = 32 * i
-            r1 = 64 + 32 * i
-            nc.scalar.copy(
-                out=sel[i][r0:r0 + 32, :].rearrange("q (a p) -> q a p", p=HW),
-                in_=ident[r0:r0 + 32, r0:r0 + 32].unsqueeze(1).broadcast_to([32, HW, HW]),
-            )
-            nc.scalar.copy(
-                out=sel[i][r1:r1 + 32, :].rearrange("q (a p) -> q a p", p=HW),
-                in_=ident[r1:r1 + 32, r1:r1 + 32].unsqueeze(2).broadcast_to([32, HW, HW]),
-            )
+        def make_select_on_scalar(i):
+            for r, axis in ((HW * i, 1), (64 + HW * i, 2)):
+                nc.scalar.copy(
+                    out=select[i][r:r + HW, :].rearrange("q (a p) -> q a p", p=HW),
+                    in_=ident[r:r + HW, r:r + HW].unsqueeze(axis).broadcast_to([HW, HW, HW]),
+                )
 
-        def add_v(c, a0, a1):
-            s = V_SAMPLES[c]
-            n = a1 - a0
-            u = u_rows(s) if s < 12 else u_sbuf(s)
+
+        def add_on_vector(c, n_a):
+            s = VECTOR_SAMPLES[c]
+            u = u_in_psum(s) if s < 3 * GROUP else u_in_sbuf(s)
             nc.vector.tensor_tensor(
-                out=pre[c % 2][:, a0 * P:a1 * P].rearrange("q (a p t) -> q a p t", p=HW, t=T),
-                in0=u.unsqueeze(1).broadcast_to([P, n, HW, T]),
-                in1=vb[:, 32 * s + a0:32 * s + a1, :].unsqueeze(2).broadcast_to([P, n, HW, T]),
+                out=pre[c % 2][:, 0:n_a * P].rearrange("q (a p t) -> q a p t", p=HW, t=T),
+                in0=u.unsqueeze(1).broadcast_to([P, n_a, HW, T]),
+                in1=vb[:, HW * s:HW * s + n_a, :].unsqueeze(2).broadcast_to([P, n_a, HW, T]),
                 op=ADD,
             )
 
-        def add_g(c):
-            s, half = G_HALVES[c]
-            a0 = 32 * s + 16 * half
-            nc.gpsimd.tensor_tensor(
-                out=hg[c % 2][:].rearrange("q (a p t) -> q a p t", p=HW, t=T),
-                in0=u_sbuf(s).unsqueeze(1).broadcast_to([P, 16, HW, T]),
-                in1=vb[:, a0:a0 + 16, :].unsqueeze(2).broadcast_to([P, 16, HW, T]),
-                op=ADD,
-            )
-
-        def relu_v(c, a0, a1):
+        def relu_on_vector(c, a0, a1):
             nc.vector.tensor_scalar_max(hv[c % 2][:, a0 * P:a1 * P], pre[c % 2][:, a0 * P:a1 * P], 0.0)
 
-        def relu_g(c):
-            if RELU_G_ON_V[c]:
-                nc.vector.tensor_scalar_max(hg[c % 2][:], hg[c % 2][:], 0.0)
-            else:
-                nc.scalar.activation(out=hg[c % 2][:], in_=hg[c % 2][:], func=RELU)
-
-        def chunk_h(k):
-            i, r = k // 8, k % 8
-            ps = tmp_bank()
-            for t in range(T):
-                nc.tensor.matmul(ps[:, t * P:(t + 1) * P], lhsT=uv[:, t * P:(t + 1) * P], rhs=sel[i][:, r * P:(r + 1) * P], start=True, stop=True)
-            return ps
-
-        def relu_h(k, ps):
-            r = k % 4
-            nc.scalar.activation(
-                out=hh[(k // 4) % 2][:, r * 512:(r + 1) * 512].rearrange("q (n t) -> q n t", t=T),
-                in_=ps[:].rearrange("q (t n) -> q n t", t=T),
-                func=RELU,
+        def add_on_gpsimd(c):
+            s, half = GPSIMD_HALVES[c]
+            a0 = HW * s + A_UNIT * half
+            nc.gpsimd.tensor_tensor(
+                out=hg[c % 2][:].rearrange("q (a p t) -> q a p t", p=HW, t=T),
+                in0=u_in_sbuf(s).unsqueeze(1).broadcast_to([P, A_UNIT, HW, T]),
+                in1=vb[:, a0:a0 + A_UNIT, :].unsqueeze(2).broadcast_to([P, A_UNIT, HW, T]),
+                op=ADD,
             )
 
-        def unit(codes, scales, s, pair, lo=0, n=512):
+        def add_and_relu_chunks(numbers):
+            made = []
+            for k in numbers:
+                i, r = k // SAMPLE_CHUNKS, k % SAMPLE_CHUNKS
+                ps = rotating_bank()
+                made.append((k, ps))
+                for t in range(T):
+                    nc.tensor.matmul(
+                        ps[:, t * CHUNK:(t + 1) * CHUNK],
+                        lhsT=uv[:, t * P:(t + 1) * P],
+                        rhs=select[i][:, r * CHUNK:(r + 1) * CHUNK],
+                        start=True,
+                        stop=True,
+                    )
+            for k, ps in made:
+                r = k % CHUNKS_A_UNIT
+                nc.scalar.activation(
+                    out=ht[k // CHUNKS_A_UNIT % 2][:, r * CHUNK * T:(r + 1) * CHUNK * T].rearrange("q (n t) -> q n t", t=T),
+                    in_=ps[:].rearrange("q (t n) -> q n t", t=T),
+                    func=RELU,
+                )
+
+
+        def unit(codes, scales, s, pair, lo=0, n=UNIT):
             return {"codes": codes[:, lo:lo + n], "scales": scales[:, lo:lo + n], "s": s, "pair": pair, "n": n}
 
-        def store(u, o):
+        def store(u, tile):
             n = u["n"]
             rows = out[u["s"]].rearrange("a p c -> (a p) c")[u["pair"]:u["pair"] + n, :]
-            nc.sync.dma_start(out=rows.rearrange("(j q) c -> q j c", q=P), in_=o[:, 0:n].rearrange("q (j c) -> q j c", c=P))
+            nc.sync.dma_start(
+                out=rows.rearrange("(j q) c -> q j c", q=P),
+                in_=tile[:, 0:n].rearrange("q (j c) -> q j c", c=G2),
+            )
 
-        def mm(u, tag):
+
+        def multiply(u, tag):
             u["y"] = bank(tag)
-            nc.tensor.matmul_mx(out=u["y"][:], lhsT=w2[:].bitcast(FP8X4), lhsT_scale=w2s[:], rhs=u["codes"].bitcast(FP8X4), rhs_scale=u["scales"], start=True, stop=True)
+            nc.tensor.matmul_mx(
+                out=u["y"][:],
+                lhsT=w2[:].bitcast(FP8X4),
+                lhsT_scale=w2s[:],
+                rhs=u["codes"].bitcast(FP8X4),
+                rhs_scale=u["scales"],
+                start=True,
+                stop=True,
+            )
 
-        def pass1(u):
-            u["ys"] = ring.tile([P, 512], F32, name="ys")
+        def bias_relu(u):
+            u["ys"] = ring.tile([P, UNIT], F32, name="ys")
             nc.scalar.activation(out=u["ys"][:], in_=u["y"][:], func=RELU, bias=b2[:, 0:1])
 
         def turn(u):
-            u["t"] = tmp_bank()
-            for j in range(4):
-                nc.tensor.transpose(u["t"][:, j * P:(j + 1) * P], u["ys"][:, j * P:(j + 1) * P], ident[:])
+            u["turned"] = rotating_bank()
+            for j in range(UNIT // P):
+                cols = slice(j * P, (j + 1) * P)
+                nc.tensor.transpose(u["turned"][:, cols], u["ys"][:, cols], ident[:])
 
-        def pass2(u):
-            o = ring.tile([P, 512], F32, name="o")
-            nc.scalar.copy(out=o[:], in_=u["t"][:])
+        def copy_and_store(u):
+            o = ring.tile([P, UNIT], F32, name="o")
+            nc.scalar.copy(out=o[:], in_=u["turned"][:])
             store(u, o)
 
-        def mm_rows(u, tag):
+
+        def multiply_rows(u, tag):
             u["y"] = bank(tag)
             for j in range(u["n"] // P):
                 cols = slice(j * P, (j + 1) * P)
-                nc.tensor.matmul_mx(out=u["y"][:, cols], lhsT=u["codes"][:, cols].bitcast(FP8X4), lhsT_scale=u["scales"][:, cols], rhs=w2[:].bitcast(FP8X4), rhs_scale=w2s[:], start=True, stop=True)
+                nc.tensor.matmul_mx(
+                    out=u["y"][:, cols],
+                    lhsT=u["codes"][:, cols].bitcast(FP8X4),
+                    lhsT_scale=u["scales"][:, cols],
+                    rhs=w2[:].bitcast(FP8X4),
+                    rhs_scale=w2s[:],
+                    start=True,
+                    stop=True,
+                )
 
-        def finish_rows(u):
+        def bias_relu_and_store_rows(u):
             n = u["n"]
-            ys = ring.tile([P, 512], F32, name="yr")
-            o = ring.tile([P, 512], F32, name="o2")
+            biased = ring.tile([P, UNIT], F32, name="biased")
+            o = ring.tile([P, UNIT], F32, name="o_rows")
             nc.vector.tensor_tensor(
-                out=ys[:, 0:n].rearrange("q (j c) -> q j c", c=P),
-                in0=u["y"][:, 0:n].rearrange("q (j c) -> q j c", c=P),
-                in1=b2row[:].unsqueeze(1).broadcast_to([P, n // P, P]),
+                out=biased[:, 0:n].rearrange("q (j c) -> q j c", c=G2),
+                in0=u["y"][:, 0:n].rearrange("q (j c) -> q j c", c=G2),
+                in1=b2row[:].unsqueeze(1).broadcast_to([P, n // P, G2]),
                 op=ADD,
             )
-            nc.vector.tensor_scalar_max(o[:, 0:n], ys[:, 0:n], 0.0)
+            nc.vector.tensor_scalar_max(o[:, 0:n], biased[:, 0:n], 0.0)
             store(u, o)
 
-        def epilogue(units, hq, c):
-            n = len(units)
-            for k, ps in [(k, chunk_h(k)) for k in hq]:
-                relu_h(k, ps)
-            ytags = ["ybank0", "ybank1", "ubank0"] if c >= Y3 else ["ybank0", "ybank1"]
-            d = len(ytags)
-            for i, u in enumerate(units[:d]):
-                mm(u, ytags[i])
+        def finish(units, tags):
+            for u, tag in zip(units, tags):
+                multiply(u, tag)
             for u in units[:2]:
-                pass1(u)
-            for i in range(n):
-                turn(units[i])
-                if i + d < n:
-                    mm(units[i + d], ytags[i])
-                if i + 2 < n and d > 2:
-                    pass1(units[i + 2])
-                pass2(units[i])
-                if i + 2 < n and d == 2:
-                    pass1(units[i + 2])
+                bias_relu(u)
+            for i, u in enumerate(units):
+                turn(u)
+                if i + len(tags) < len(units):
+                    multiply(units[i + len(tags)], tags[i])
+                ahead = units[i + 2:i + 3]
+                if len(tags) > 2:
+                    for v in ahead:
+                        bias_relu(v)
+                copy_and_store(u)
+                if len(tags) == 2:
+                    for v in ahead:
+                        bias_relu(v)
 
         with tc.manual_schedule():
-            nc.scalar.dma_start(out=scale[:], in_=x_scale.rearrange("o (g q t) z -> q (o g) (t z)", q=P, t=T))
-            nc.scalar.dma_start(out=b1[:], in_=g1_b.rearrange("(q t) -> q t", t=T))
-            nc.scalar.dma_start(out=b2[:], in_=g2_b.rearrange("(q o) -> q o", o=1))
-            nc.vector.memset(warm[:], 0.0)
+            nc.scalar.dma_start(out=x_scales[:], in_=x_scale.rearrange("o (g q t) z -> q (o g) (t z)", q=P, t=T))
+            nc.vector.memset(warm_in[:], 0.0)
             nc.vector.memset(w1s[:].bitcast(I32), 0)
             nc.vector.memset(w2s[:].bitcast(I32), 0)
-            nc.vector.memset(sel[1][:], 0.0)
-            nc.scalar.activation(out=warm2[:], in_=warm[:], func=RELU)
-            make_sel_g(0)
-            make_sel_s(1)
+            nc.vector.memset(select[1][:], 0.0)
+            nc.scalar.activation(out=warm_out[:], in_=warm_in[:], func=RELU)
+            make_select_on_gpsimd(0)
+            make_select_on_scalar(1)
+            nc.scalar.dma_start(out=b1[:], in_=g1_b.rearrange("(q t) -> q t", t=T))
             load_x(0)
-            for q in range(4):
-                nc.sync.dma_start(out=w1s[32 * q:32 * q + 16, :].bitcast(I32), in_=g1_w_scales[:, 4 * q:4 * q + 4, :].bitcast(I32))
-            for g in (2, 3, 0, 1):
-                nc.sync.dma_start(out=w1[g][:].bitcast(I32), in_=g1_w_words[g].rearrange("q n t -> q (n t)").bitcast(I32))
+            for quadrant in range(4):
+                nc.sync.dma_start(
+                    out=w1s[32 * quadrant:32 * quadrant + 16, :].bitcast(I32),
+                    in_=g1_w_scales[:, 4 * quadrant:4 * quadrant + 4, :].bitcast(I32),
+                )
+            for i in (1, 0):
+                nc.sync.dma_start(
+                    out=w1[i][:].bitcast(I32).rearrange("q (g n) -> q g n", g=2),
+                    in_=g1_w_words[2 * i:2 * i + 2].rearrange("g q n t -> q g (n t)").bitcast(I32),
+                )
             load_x(3)
             load_x(1)
             load_x(2)
             nc.sync.dma_start(out=w2[:].bitcast(I32), in_=g2_w_words[0].rearrange("q n t -> q (n t)").bitcast(I32))
-            for q in range(4):
-                nc.sync.dma_start(out=w2s[32 * q:32 * q + 4, :].bitcast(I32), in_=g2_w_scales[0, 4 * q:4 * q + 4, :].bitcast(I32))
-
-            cast_on_vector(0)
-            scale_on_vector(0)
-            quant_x(0)
-            nc.vector.tensor_copy(out=w1sp[:].rearrange("q (t m) -> q t m", t=T), in_=w1s[:].rearrange("q (m t) -> q t m", t=T))
-            for g in (2, 3, 0, 1):
-                nc.vector.tensor_copy(
-                    out=w1p[g][:].bitcast(I32).rearrange("q (t m) -> q t m", t=T),
-                    in_=w1[g][:].bitcast(I32).rearrange("q (m t) -> q t m", t=T),
+            for quadrant in range(4):
+                nc.sync.dma_start(
+                    out=w2s[32 * quadrant:32 * quadrant + 4, :].bitcast(I32),
+                    in_=g2_w_scales[0, 4 * quadrant:4 * quadrant + 4, :].bitcast(I32),
                 )
+
+            widen_on_vector(0)
+            scale_on_vector(0)
+            quantize_x(0)
+            for i in (1, 0):
+                nc.vector.tensor_copy(
+                    out=w1p[i][:].bitcast(I32).rearrange("q (g t m) -> q g t m", g=2, t=T),
+                    in_=w1[i][:].bitcast(I32).rearrange("q (g m t) -> q g t m", g=2, t=T),
+                )
+                if i == 1:
+                    nc.vector.tensor_copy(
+                        out=w1sp[:].rearrange("q (t m) -> q t m", t=T),
+                        in_=w1s[:].rearrange("q (m t) -> q t m", t=T),
+                    )
             nc.scalar.dma_start(out=b1row[64:128, :], in_=g1_b.partition_broadcast(64))
-            cast_x(3)
+            widen_on_scalar(3)
             make_v(0)
-            bias_v(0, 0, 112)
+            add_bias_1(0, 0, P - A_UNIT)
             make_u(0)
-            if not ON_V[3]:
-                scale_on_scalar(3)
-            cast_x(1)
-            cast_x(2)
+            scale_on_scalar(3)
+            widen_on_scalar(1)
+            widen_on_scalar(2)
+            nc.scalar.dma_start(out=b2[:], in_=g2_b.rearrange("(q o) -> q o", o=1))
             nc.scalar.dma_start(out=b2row[:], in_=g2_b.partition_broadcast(P))
 
-            last = len(V_SAMPLES) - 1
-            h_ready = []
-            for c in range(last):
+            tensor_ready = []
+            for c in range(STEPS):
                 k = c - 1
                 units = []
-                add_v(c, 0, 32)
-                add_g(c)
-                if c == 1:
-                    bias_v(3, 64, 128)
-                for j in (1, 2):
-                    if c == j:
-                        if ON_V[j]:
-                            scale_on_vector(j)
-                        quant_x(j)
+                add_on_vector(c, HW)
+                add_on_gpsimd(c)
                 if c == 0:
-                    if ON_V[3]:
-                        scale_on_vector(3)
-                    quant_x(3)
-                    bias_v(0, 112, P)
-                    make_uv_h()
+                    quantize_x(3)
+                    add_bias_1(0, P - A_UNIT, P)
+                    make_uv()
                     make_u(3)
                     make_v(3)
-                else:
-                    if RELU_G_ON_V[k]:
-                        relu_g(k)
-                    quant(cv[k % 2][:], sv[k % 2][:], hv[k % 2][:])
-                    units += [unit(cv[k % 2], sv[k % 2], V_SAMPLES[k], 512 * half, 512 * half) for half in range(2)]
-                for n in h_ready:
-                    quant(ch[n % 2][:], sh[n % 2][:], hh[n % 2][:])
-                    units.append(unit(ch[n % 2], sh[n % 2], H_SAMPLES[n // 2], n % 2 * 512))
-                if c >= 1:
-                    quant(cg[k % 2][:], sg[k % 2][:], hg[k % 2][:])
-                    units.append(unit(cg[k % 2], sg[k % 2], G_HALVES[k][0], 512 * G_HALVES[k][1]))
-                relu_v(c, 0, 32)
-                if not RELU_G_ON_V[c]:
-                    relu_g(c)
+                elif c == 1:
+                    add_bias_1(3, 64, P)
+                    scale_on_vector(1)
+                    quantize_x(1)
+                elif c == 2:
+                    quantize_x(2)
+                if c > 0:
+                    if k > LAST_SCALAR_RELU:
+                        nc.vector.tensor_scalar_max(hg[k % 2][:], hg[k % 2][:], 0.0)
+                    quantize(cv[k % 2][:], sv[k % 2][:], hv[k % 2][:])
+                    units += [unit(cv[k % 2], sv[k % 2], VECTOR_SAMPLES[k], lo, lo) for lo in (0, UNIT)]
+                for n in tensor_ready:
+                    quantize(ct[n % 2][:], st[n % 2][:], ht[n % 2][:])
+                    units.append(unit(ct[n % 2], st[n % 2], TENSOR_SAMPLES[n // 2], n % 2 * UNIT))
+                if c > 0:
+                    quantize(cg[k % 2][:], sg[k % 2][:], hg[k % 2][:])
+                    units.append(unit(cg[k % 2], sg[k % 2], GPSIMD_HALVES[k][0], GPSIMD_HALVES[k][1] * UNIT))
+                relu_on_vector(c, 0, HW)
+                if c <= LAST_SCALAR_RELU:
+                    nc.scalar.activation(out=hg[c % 2][:], in_=hg[c % 2][:], func=RELU)
                 if c == 0:
-                    bias_v_h()
-                    for j in (1, 2):
-                        if not ON_V[j]:
-                            scale_on_scalar(j)
-                elif c in (1, 2):
+                    add_bias_1_rows()
+                    scale_on_scalar(2)
+                elif c < 3:
                     make_u(c)
                     make_v(c)
-                    bias_v(c, 0, P)
-                done = sum(H_CHUNKS[:c])
-                hq = list(range(done, done + H_CHUNKS[c]))
-                h_ready = [n // 4 for n in hq if n % 4 == 3]
-                epilogue(units, hq, c)
+                    add_bias_1(c, 0, P)
+                numbers = list(range(c * CHUNKS_A_STEP, (c + 1) * CHUNKS_A_STEP))
+                numbers = [n for n in numbers if n < len(TENSOR_SAMPLES) * SAMPLE_CHUNKS]
+                add_and_relu_chunks(numbers)
+                tensor_ready = [n // CHUNKS_A_UNIT for n in numbers if n % CHUNKS_A_UNIT == CHUNKS_A_UNIT - 1]
+                free = ["u_of_group_0"] if c >= FREE_BANK_STEP else []
+                finish(units, ["y0", "y1"] + free)
 
-            k = last - 1
-            add_v(last, 0, 16)
-            quant(cg[k % 2][:], sg[k % 2][:], hg[k % 2][:])
-            quant(cv[k % 2][:], sv[k % 2][:], hv[k % 2][:])
-            relu_v(last, 0, 8)
-            relu_v(last, 8, 16)
-            for half in range(2):
-                quant(cv[last % 2][:, half * 256:(half + 1) * 256], sv[last % 2][:, half * 256:(half + 1) * 256], hv[last % 2][:, half * 1024:(half + 1) * 1024])
-            tail = [unit(cg[k % 2], sg[k % 2], G_HALVES[k][0], 512 * G_HALVES[k][1])]
-            tail += [unit(cv[k % 2], sv[k % 2], V_SAMPLES[k], 512 * half, 512 * half) for half in range(2)]
-            tail += [unit(cv[last % 2], sv[last % 2], V_SAMPLES[last], 256 * half, 256 * half, 256) for half in range(2)]
-            mm(tail[0], TAIL_TAGS[0])
-            mm(tail[1], TAIL_TAGS[1])
-            mm_rows(tail[2], TAIL_TAGS[2])
-            pass1(tail[0])
-            turn(tail[0])
-            pass1(tail[1])
-            pass2(tail[0])
-            mm_rows(tail[3], TAIL_TAGS[3])
-            mm_rows(tail[4], TAIL_TAGS[4])
-            turn(tail[1])
-            pass2(tail[1])
-            finish_rows(tail[2])
-            finish_rows(tail[3])
-            finish_rows(tail[4])
+            k = STEPS - 1
+            c = STEPS
+            quarter = UNIT // 2
+            add_on_vector(c, A_UNIT)
+            if k > LAST_SCALAR_RELU:
+                nc.vector.tensor_scalar_max(hg[k % 2][:], hg[k % 2][:], 0.0)
+            quantize(cg[k % 2][:], sg[k % 2][:], hg[k % 2][:])
+            quantize(cv[k % 2][:], sv[k % 2][:], hv[k % 2][:])
+            for i in range(2):
+                relu_on_vector(c, i * A_UNIT // 2, (i + 1) * A_UNIT // 2)
+            for lo in (0, quarter):
+                quantize(cv[c % 2][:, lo:lo + quarter], sv[c % 2][:, lo:lo + quarter], hv[c % 2][:, lo * T:(lo + quarter) * T])
+            first = unit(cg[k % 2], sg[k % 2], GPSIMD_HALVES[k][0], GPSIMD_HALVES[k][1] * UNIT)
+            second, third = [unit(cv[k % 2], sv[k % 2], VECTOR_SAMPLES[k], lo, lo) for lo in (0, UNIT)]
+            fourth, fifth = [unit(cv[c % 2], sv[c % 2], VECTOR_SAMPLES[c], lo, lo, quarter) for lo in (0, quarter)]
+            multiply(first, "y0")
+            multiply(second, "y1")
+            multiply_rows(third, "u_of_group_0")
+            bias_relu(first)
+            turn(first)
+            bias_relu(second)
+            copy_and_store(first)
+            multiply_rows(fourth, "u_of_group_1")
+            multiply_rows(fifth, "u_of_group_2")
+            turn(second)
+            copy_and_store(second)
+            bias_relu_and_store_rows(third)
+            bias_relu_and_store_rows(fourth)
+            bias_relu_and_store_rows(fifth)

from contextlib import ExitStack

import concourse.mybir as mybir
from concourse.masks import make_identity

F32 = mybir.dt.float32
BF16 = mybir.dt.bfloat16
U32 = mybir.dt.uint32
I32 = mybir.dt.int32
U8 = mybir.dt.uint8
FP8 = mybir.dt.float8_e4m3fn
FP8X4 = mybir.dt.float8_e4m3fn_x4
ADD = mybir.AluOpType.add
MULT = mybir.AluOpType.mult
COPY = mybir.ActivationFunctionType.Copy
RELU = mybir.ActivationFunctionType.Relu

MB, C, HW, K1, G2 = 16, 1024, 32, 512, 128
P = 128
T = 4
GROUP = 4
PAIRS = HW * HW
UNIT = 512
A_UNIT = UNIT // HW
BANK = 512
CHUNK = 128

FLOPS = 2 * MB * HW * C * K1 * 2 + 2 * MB * PAIRS * K1 * G2

VECTOR_SAMPLES = [0, 1, 2, 4, 5, 6, 8, 9, 10, 14]
GPSIMD_HALVES = [(3, 0), (3, 1), (7, 0), (7, 1), (11, 0), (11, 1), (15, 0), (15, 1), (14, 1)]
TENSOR_SAMPLES = [12, 13]
STEPS = len(GPSIMD_HALVES)
CHUNKS_A_STEP = 2
CHUNKS_A_UNIT = UNIT // CHUNK
SAMPLE_CHUNKS = PAIRS // CHUNK
LAST_SCALAR_RELU = STEPS - 3
FREE_BANK_STEP = 3


def tile_reidrnself_pa_t_w8_kernel(tc, x_bytes, x_scale, g1_w_words, g1_w_scales, g1_b, g2_w_words, g2_w_scales, g2_b, out):
    nc = tc.nc
    with ExitStack() as ctx:
        keep = ctx.enter_context(tc.tile_pool(name="keep", bufs=1))
        ring = ctx.enter_context(tc.tile_pool(name="ring", bufs=6))
        psum = ctx.enter_context(tc.psum_pool(name="psum", bufs=1))

        ident = keep.tile([P, P], F32, name="ident")
        make_identity(nc, ident[:])

        xb = [keep.tile([P, 2 * GROUP * P], U8, name="xb%d" % j) for j in range(4)]
        xw = [keep.tile([P, 2 * GROUP * P], BF16, name="xw%d" % j) for j in range(4)]
        xg = [keep.tile([P, 2 * P * T], BF16, name="xg%d" % j, align_bytes=64) for j in range(4)]
        xc03 = keep.tile([P, 4 * P], U32, name="xc03", align_bytes=64)
        xs03 = keep.tile([P, 4 * P], U8, name="xs03", align_bytes=64)
        xc12 = [keep.tile([P, 2 * P], U32, name="xc%d" % j, align_bytes=64) for j in (1, 2)]
        xs12 = [keep.tile([P, 2 * P], U8, name="xs%d" % j, align_bytes=64) for j in (1, 2)]
        x_scales = keep.tile([P, 2, T], F32, name="x_scales")

        w1 = [keep.tile([P, 2 * K1], U32, name="w1raw%d" % i) for i in range(2)]
        w1p = [keep.tile([P, 2 * K1], U32, name="w1p%d" % i, align_bytes=64) for i in range(2)]
        w1s = keep.tile([P, K1], U8, name="w1s")
        w1sp = keep.tile([P, K1], U8, name="w1sp", align_bytes=64)
        w2 = keep.tile([P, G2], U32, name="w2", align_bytes=64)
        w2s = keep.tile([P, G2], U8, name="w2s", align_bytes=64)
        b1 = keep.tile([P, T], BF16, name="b1")
        b1row = keep.tile([P, K1], BF16, name="b1row")
        b2 = keep.tile([P, 1], BF16, name="b2")
        b2row = keep.tile([P, G2], BF16, name="b2row")

        vb = keep.tile([P, MB * HW, T], F32, name="vb", align_bytes=64)
        usb = [keep.tile([P, 2 * HW, T], F32, name="usb%d" % j, align_bytes=64) for j in range(4)]
        uv = keep.tile([P, K1], F32, name="uv")
        select = [keep.tile([P, PAIRS], F32, name="select%d" % i) for i in range(2)]

        pre = [keep.tile([P, PAIRS * T], BF16, name="pre%d" % i, align_bytes=64) for i in range(2)]
        hv = [keep.tile([P, PAIRS * T], BF16, name="hv%d" % i, align_bytes=64) for i in range(2)]
        hg = [keep.tile([P, UNIT * T], BF16, name="hg%d" % i, align_bytes=64) for i in range(2)]
        ht = [keep.tile([P, UNIT * T], BF16, name="ht%d" % i, align_bytes=64) for i in range(2)]
        cv = [keep.tile([P, PAIRS], U32, name="cv%d" % i, align_bytes=64) for i in range(2)]
        sv = [keep.tile([P, PAIRS], U8, name="sv%d" % i, align_bytes=64) for i in range(2)]
        cg = [keep.tile([P, UNIT], U32, name="cg%d" % i, align_bytes=64) for i in range(2)]
        sg = [keep.tile([P, UNIT], U8, name="sg%d" % i, align_bytes=64) for i in range(2)]
        ct = [keep.tile([P, UNIT], U32, name="ct%d" % i, align_bytes=64) for i in range(2)]
        st = [keep.tile([P, UNIT], U8, name="st%d" % i, align_bytes=64) for i in range(2)]
        warm_in = keep.tile([P, 1], F32, name="warm_in")
        warm_out = keep.tile([P, 1], F32, name="warm_out")

        banks_made = []

        def bank(tag, bufs=1):
            banks_made.append(tag)
            return psum.tile([P, BANK], F32, name="%s_%d" % (tag, len(banks_made)), tag=tag, bufs=bufs)

        def rotating_bank():
            return bank("rotating", 3)

        u_bank = {}
        v_bank = {}


        def load_x(j):
            nc.sync.dma_start(
                out=xb[j][:].rearrange("q (b n) -> q b n", b=2 * GROUP),
                in_=x_bytes[GROUP * j:GROUP * (j + 1)].rearrange("b (g q t) n -> q (b g) (t n)", g=2, t=T),
            )

        def widen_on_scalar(j):
            nc.scalar.copy(out=xw[j][:], in_=xb[j][:].bitcast(FP8))

        def widen_on_vector(j):
            nc.vector.tensor_copy(out=xw[j][:], in_=xb[j][:].bitcast(FP8))

        def widened(j, g):
            return xw[j][:].rearrange("q (b g t n) -> q g b n t", b=GROUP, g=2, t=T)[:, g]

        def scaled(j, g):
            return xg[j][:, g * P * T:(g + 1) * P * T].rearrange("q (b n t) -> q b n t", b=GROUP, t=T)

        def scale_on_scalar(j):
            for g in range(2):
                for t in range(T):
                    nc.scalar.activation(
                        out=scaled(j, g)[:, :, :, t],
                        in_=widened(j, g)[:, :, :, t],
                        func=COPY,
                        scale=x_scales[:, g, t:t + 1],
                    )

        def scale_on_vector(j):
            for g in range(2):
                nc.vector.tensor_tensor(
                    out=scaled(j, g),
                    in0=widened(j, g),
                    in1=x_scales[:, g, :].unsqueeze(1).unsqueeze(1).broadcast_to([P, GROUP, HW, T]),
                    op=MULT,
                )

        def quantize(codes, scales, values):
            nc.vector.quantize_mx(out=codes.bitcast(FP8X4), scales=scales, in_=values)

        def x_operand(j, g, shift=0):
            if j in (0, 3):
                lo = 2 * P * g + (P if j == 3 else 0) + shift
                return xc03[:, lo:lo + P], xs03[:, lo:lo + P]
            return xc12[j - 1][:, g * P:(g + 1) * P], xs12[j - 1][:, g * P:(g + 1) * P]

        def quantize_x(j):
            if j in (0, 3):
                for g in range(2):
                    codes, scales = x_operand(j, g)
                    quantize(codes, scales, xg[j][:, g * P * T:(g + 1) * P * T])
            else:
                quantize(xc12[j - 1][:], xs12[j - 1][:], xg[j][:])


        def w1_operand(w, lo, n):
            return w1p[w // 2][:, w % 2 * K1 + lo:w % 2 * K1 + lo + n], w1sp[4 * w:P, lo:lo + n]

        def channels_on_partitions(j, ps, first_w):
            for t in range(T):
                for g in range(2):
                    w_codes, w_scales = w1_operand(first_w + g, t * P, P)
                    codes, scales = x_operand(j, g)
                    nc.tensor.matmul_mx(
                        out=ps[:, t * P:(t + 1) * P],
                        lhsT=w_codes.bitcast(FP8X4),
                        lhsT_scale=w_scales,
                        rhs=codes.bitcast(FP8X4),
                        rhs_scale=scales,
                        start=(g == 0),
                        stop=(g == 1),
                    )

        def rows_on_partitions(ps, first_w, shift):
            for g in range(2):
                w_codes, w_scales = w1_operand(first_w + g, 0, K1)
                codes, scales = x_operand(3, g, shift)
                nc.tensor.matmul_mx(
                    out=ps[:],
                    lhsT=codes.bitcast(FP8X4),
                    lhsT_scale=scales,
                    rhs=w_codes.bitcast(FP8X4),
                    rhs_scale=w_scales,
                    start=(g == 0),
                    stop=(g == 1),
                )

        def u_in_psum(s, n=HW):
            r = HW * (s % GROUP)
            return u_bank[s // GROUP][:].rearrange("q (t r) -> q r t", t=T)[:, r:r + n, :]

        def u_in_sbuf(s):
            r = HW * (s % 2) if s >= 3 * GROUP else 0
            return usb[s // GROUP][:, r:r + HW, :]

        def make_u(j):
            u_bank[j] = bank("u_of_group_%d" % j) if j < 3 else rotating_bank()
            channels_on_partitions(j, u_bank[j], 0)
            if j < 3:
                nc.scalar.copy(out=usb[j][:, 0:HW, :], in_=u_in_psum(GROUP * j + 3))
            else:
                nc.scalar.copy(out=usb[j][:], in_=u_in_psum(14, 2 * HW))

        def make_v(j):
            v_bank[j] = rotating_bank()
            channels_on_partitions(j, v_bank[j], 2)

        def add_bias_1(j, r0, r1):
            nc.vector.tensor_tensor(
                out=vb[:, j * P + r0:j * P + r1, :],
                in0=v_bank[j][:].rearrange("q (t r) -> q r t", t=T)[:, r0:r1, :],
                in1=b1[:].unsqueeze(1).broadcast_to([P, r1 - r0, T]),
                op=ADD,
            )

        def make_uv():
            ps = rotating_bank()
            rows_on_partitions(ps, 0, 0)
            nc.scalar.copy(out=uv[0:64, :], in_=ps[0:64, :])
            v_bank["rows"] = rotating_bank()
            rows_on_partitions(v_bank["rows"], 2, -64)

        def add_bias_1_rows():
            nc.vector.tensor_tensor(
                out=uv[64:128, :].rearrange("q (t m) -> q t m", t=T),
                in0=v_bank["rows"][64:128, :].rearrange("q (t m) -> q t m", t=T),
                in1=b1row[64:128, :].rearrange("q (m t) -> q t m", t=T),
                op=ADD,
            )


        def make_select_on_gpsimd(i):
            nc.gpsimd.tensor_tensor(
                out=select[i][:].rearrange("q (a p) -> q a p", p=HW),
                in0=ident[:, HW * i:HW * (i + 1)].unsqueeze(1).broadcast_to([P, HW, HW]),
                in1=ident[:, 64 + HW * i:64 + HW * (i + 1)].unsqueeze(2).broadcast_to([P, HW, HW]),
                op=ADD,
            )

        def make_select_on_scalar(i):
            for r, axis in ((HW * i, 1), (64 + HW * i, 2)):
                nc.scalar.copy(
                    out=select[i][r:r + HW, :].rearrange("q (a p) -> q a p", p=HW),
                    in_=ident[r:r + HW, r:r + HW].unsqueeze(axis).broadcast_to([HW, HW, HW]),
                )


        def add_on_vector(c, n_a):
            s = VECTOR_SAMPLES[c]
            u = u_in_psum(s) if s < 3 * GROUP else u_in_sbuf(s)
            nc.vector.tensor_tensor(
                out=pre[c % 2][:, 0:n_a * P].rearrange("q (a p t) -> q a p t", p=HW, t=T),
                in0=u.unsqueeze(1).broadcast_to([P, n_a, HW, T]),
                in1=vb[:, HW * s:HW * s + n_a, :].unsqueeze(2).broadcast_to([P, n_a, HW, T]),
                op=ADD,
            )

        def relu_on_vector(c, a0, a1):
            nc.vector.tensor_scalar_max(hv[c % 2][:, a0 * P:a1 * P], pre[c % 2][:, a0 * P:a1 * P], 0.0)

        def add_on_gpsimd(c):
            s, half = GPSIMD_HALVES[c]
            a0 = HW * s + A_UNIT * half
            nc.gpsimd.tensor_tensor(
                out=hg[c % 2][:].rearrange("q (a p t) -> q a p t", p=HW, t=T),
                in0=u_in_sbuf(s).unsqueeze(1).broadcast_to([P, A_UNIT, HW, T]),
                in1=vb[:, a0:a0 + A_UNIT, :].unsqueeze(2).broadcast_to([P, A_UNIT, HW, T]),
                op=ADD,
            )

        def add_and_relu_chunks(numbers):
            made = []
            for k in numbers:
                i, r = k // SAMPLE_CHUNKS, k % SAMPLE_CHUNKS
                ps = rotating_bank()
                made.append((k, ps))
                for t in range(T):
                    nc.tensor.matmul(
                        ps[:, t * CHUNK:(t + 1) * CHUNK],
                        lhsT=uv[:, t * P:(t + 1) * P],
                        rhs=select[i][:, r * CHUNK:(r + 1) * CHUNK],
                        start=True,
                        stop=True,
                    )
            for k, ps in made:
                r = k % CHUNKS_A_UNIT
                nc.scalar.activation(
                    out=ht[k // CHUNKS_A_UNIT % 2][:, r * CHUNK * T:(r + 1) * CHUNK * T].rearrange("q (n t) -> q n t", t=T),
                    in_=ps[:].rearrange("q (t n) -> q n t", t=T),
                    func=RELU,
                )


        def unit(codes, scales, s, pair, lo=0, n=UNIT):
            return {"codes": codes[:, lo:lo + n], "scales": scales[:, lo:lo + n], "s": s, "pair": pair, "n": n}

        def store(u, tile):
            n = u["n"]
            rows = out[u["s"]].rearrange("a p c -> (a p) c")[u["pair"]:u["pair"] + n, :]
            nc.sync.dma_start(
                out=rows.rearrange("(j q) c -> q j c", q=P),
                in_=tile[:, 0:n].rearrange("q (j c) -> q j c", c=G2),
            )


        def multiply(u, tag):
            u["y"] = bank(tag)
            nc.tensor.matmul_mx(
                out=u["y"][:],
                lhsT=w2[:].bitcast(FP8X4),
                lhsT_scale=w2s[:],
                rhs=u["codes"].bitcast(FP8X4),
                rhs_scale=u["scales"],
                start=True,
                stop=True,
            )

        def bias_relu(u):
            u["ys"] = ring.tile([P, UNIT], F32, name="ys")
            nc.scalar.activation(out=u["ys"][:], in_=u["y"][:], func=RELU, bias=b2[:, 0:1])

        def turn(u):
            u["turned"] = rotating_bank()
            for j in range(UNIT // P):
                cols = slice(j * P, (j + 1) * P)
                nc.tensor.transpose(u["turned"][:, cols], u["ys"][:, cols], ident[:])

        def copy_and_store(u):
            o = ring.tile([P, UNIT], F32, name="o")
            nc.scalar.copy(out=o[:], in_=u["turned"][:])
            store(u, o)


        def multiply_rows(u, tag):
            u["y"] = bank(tag)
            for j in range(u["n"] // P):
                cols = slice(j * P, (j + 1) * P)
                nc.tensor.matmul_mx(
                    out=u["y"][:, cols],
                    lhsT=u["codes"][:, cols].bitcast(FP8X4),
                    lhsT_scale=u["scales"][:, cols],
                    rhs=w2[:].bitcast(FP8X4),
                    rhs_scale=w2s[:],
                    start=True,
                    stop=True,
                )

        def bias_relu_and_store_rows(u):
            n = u["n"]
            biased = ring.tile([P, UNIT], F32, name="biased")
            o = ring.tile([P, UNIT], F32, name="o_rows")
            nc.vector.tensor_tensor(
                out=biased[:, 0:n].rearrange("q (j c) -> q j c", c=G2),
                in0=u["y"][:, 0:n].rearrange("q (j c) -> q j c", c=G2),
                in1=b2row[:].unsqueeze(1).broadcast_to([P, n // P, G2]),
                op=ADD,
            )
            nc.vector.tensor_scalar_max(o[:, 0:n], biased[:, 0:n], 0.0)
            store(u, o)

        def finish(units, tags):
            for u, tag in zip(units, tags):
                multiply(u, tag)
            for u in units[:2]:
                bias_relu(u)
            for i, u in enumerate(units):
                turn(u)
                if i + len(tags) < len(units):
                    multiply(units[i + len(tags)], tags[i])
                ahead = units[i + 2:i + 3]
                if len(tags) > 2:
                    for v in ahead:
                        bias_relu(v)
                copy_and_store(u)
                if len(tags) == 2:
                    for v in ahead:
                        bias_relu(v)

        with tc.manual_schedule():
            nc.scalar.dma_start(out=x_scales[:], in_=x_scale.rearrange("o (g q t) z -> q (o g) (t z)", q=P, t=T))
            nc.vector.memset(warm_in[:], 0.0)
            nc.vector.memset(w1s[:].bitcast(I32), 0)
            nc.vector.memset(w2s[:].bitcast(I32), 0)
            nc.vector.memset(select[1][:], 0.0)
            nc.scalar.activation(out=warm_out[:], in_=warm_in[:], func=RELU)
            make_select_on_gpsimd(0)
            make_select_on_scalar(1)
            nc.scalar.dma_start(out=b1[:], in_=g1_b.rearrange("(q t) -> q t", t=T))
            load_x(0)
            for quadrant in range(4):
                nc.sync.dma_start(
                    out=w1s[32 * quadrant:32 * quadrant + 16, :].bitcast(I32),
                    in_=g1_w_scales[:, 4 * quadrant:4 * quadrant + 4, :].bitcast(I32),
                )
            for i in (1, 0):
                nc.sync.dma_start(
                    out=w1[i][:].bitcast(I32).rearrange("q (g n) -> q g n", g=2),
                    in_=g1_w_words[2 * i:2 * i + 2].rearrange("g q n t -> q g (n t)").bitcast(I32),
                )
            load_x(3)
            load_x(1)
            load_x(2)
            nc.sync.dma_start(out=w2[:].bitcast(I32), in_=g2_w_words[0].rearrange("q n t -> q (n t)").bitcast(I32))
            for quadrant in range(4):
                nc.sync.dma_start(
                    out=w2s[32 * quadrant:32 * quadrant + 4, :].bitcast(I32),
                    in_=g2_w_scales[0, 4 * quadrant:4 * quadrant + 4, :].bitcast(I32),
                )

            widen_on_vector(0)
            scale_on_vector(0)
            quantize_x(0)
            for i in (1, 0):
                nc.vector.tensor_copy(
                    out=w1p[i][:].bitcast(I32).rearrange("q (g t m) -> q g t m", g=2, t=T),
                    in_=w1[i][:].bitcast(I32).rearrange("q (g m t) -> q g t m", g=2, t=T),
                )
                if i == 1:
                    nc.vector.tensor_copy(
                        out=w1sp[:].rearrange("q (t m) -> q t m", t=T),
                        in_=w1s[:].rearrange("q (m t) -> q t m", t=T),
                    )
            nc.scalar.dma_start(out=b1row[64:128, :], in_=g1_b.partition_broadcast(64))
            widen_on_scalar(3)
            make_v(0)
            add_bias_1(0, 0, P - A_UNIT)
            make_u(0)
            scale_on_scalar(3)
            widen_on_scalar(1)
            widen_on_scalar(2)
            nc.scalar.dma_start(out=b2[:], in_=g2_b.rearrange("(q o) -> q o", o=1))
            nc.scalar.dma_start(out=b2row[:], in_=g2_b.partition_broadcast(P))

            tensor_ready = []
            for c in range(STEPS):
                k = c - 1
                units = []
                add_on_vector(c, HW)
                add_on_gpsimd(c)
                if c == 0:
                    quantize_x(3)
                    add_bias_1(0, P - A_UNIT, P)
                    make_uv()
                    make_u(3)
                    make_v(3)
                elif c == 1:
                    add_bias_1(3, 64, P)
                    scale_on_vector(1)
                    quantize_x(1)
                elif c == 2:
                    quantize_x(2)
                if c > 0:
                    if k > LAST_SCALAR_RELU:
                        nc.vector.tensor_scalar_max(hg[k % 2][:], hg[k % 2][:], 0.0)
                    quantize(cv[k % 2][:], sv[k % 2][:], hv[k % 2][:])
                    units += [unit(cv[k % 2], sv[k % 2], VECTOR_SAMPLES[k], lo, lo) for lo in (0, UNIT)]
                for n in tensor_ready:
                    quantize(ct[n % 2][:], st[n % 2][:], ht[n % 2][:])
                    units.append(unit(ct[n % 2], st[n % 2], TENSOR_SAMPLES[n // 2], n % 2 * UNIT))
                if c > 0:
                    quantize(cg[k % 2][:], sg[k % 2][:], hg[k % 2][:])
                    units.append(unit(cg[k % 2], sg[k % 2], GPSIMD_HALVES[k][0], GPSIMD_HALVES[k][1] * UNIT))
                relu_on_vector(c, 0, HW)
                if c <= LAST_SCALAR_RELU:
                    nc.scalar.activation(out=hg[c % 2][:], in_=hg[c % 2][:], func=RELU)
                if c == 0:
                    add_bias_1_rows()
                    scale_on_scalar(2)
                elif c < 3:
                    make_u(c)
                    make_v(c)
                    add_bias_1(c, 0, P)
                numbers = list(range(c * CHUNKS_A_STEP, (c + 1) * CHUNKS_A_STEP))
                numbers = [n for n in numbers if n < len(TENSOR_SAMPLES) * SAMPLE_CHUNKS]
                add_and_relu_chunks(numbers)
                tensor_ready = [n // CHUNKS_A_UNIT for n in numbers if n % CHUNKS_A_UNIT == CHUNKS_A_UNIT - 1]
                free = ["u_of_group_0"] if c >= FREE_BANK_STEP else []
                finish(units, ["y0", "y1"] + free)

            k = STEPS - 1
            c = STEPS
            quarter = UNIT // 2
            add_on_vector(c, A_UNIT)
            if k > LAST_SCALAR_RELU:
                nc.vector.tensor_scalar_max(hg[k % 2][:], hg[k % 2][:], 0.0)
            quantize(cg[k % 2][:], sg[k % 2][:], hg[k % 2][:])
            quantize(cv[k % 2][:], sv[k % 2][:], hv[k % 2][:])
            for i in range(2):
                relu_on_vector(c, i * A_UNIT // 2, (i + 1) * A_UNIT // 2)
            for lo in (0, quarter):
                quantize(cv[c % 2][:, lo:lo + quarter], sv[c % 2][:, lo:lo + quarter], hv[c % 2][:, lo * T:(lo + quarter) * T])
            first = unit(cg[k % 2], sg[k % 2], GPSIMD_HALVES[k][0], GPSIMD_HALVES[k][1] * UNIT)
            second, third = [unit(cv[k % 2], sv[k % 2], VECTOR_SAMPLES[k], lo, lo) for lo in (0, UNIT)]
            fourth, fifth = [unit(cv[c % 2], sv[c % 2], VECTOR_SAMPLES[c], lo, lo, quarter) for lo in (0, quarter)]
            multiply(first, "y0")
            multiply(second, "y1")
            multiply_rows(third, "u_of_group_0")
            bias_relu(first)
            turn(first)
            bias_relu(second)
            copy_and_store(first)
            multiply_rows(fourth, "u_of_group_1")
            multiply_rows(fifth, "u_of_group_2")
            turn(second)
            copy_and_store(second)
            bias_relu_and_store_rows(third)
            bias_relu_and_store_rows(fourth)
            bias_relu_and_store_rows(fifth)
